import numpy as np
import ml_dtypes


def mxq(x, axis, fmt="e4m3"):
    dtype, down = {"e4m3": (ml_dtypes.float8_e4m3fn, 7), "e5m2": (ml_dtypes.float8_e5m2, 14)}[fmt]
    v = np.moveaxis(np.asarray(x, np.float32).astype(ml_dtypes.bfloat16).astype(np.float64), axis, -1)
    blocks = v.reshape(v.shape[:-1] + (-1, 32))
    amax = np.abs(blocks).max(-1, keepdims=True)
    byte = np.maximum(np.where(amax > 0, np.frexp(amax)[1] - 1 + 127, 0) - down, 1)
    scale = np.exp2(byte - 127.0)
    codes = (blocks / scale).astype(np.float32).astype(dtype).astype(np.float64)
    return np.moveaxis((codes * scale).reshape(v.shape), -1, axis)


WIDE = False


def mx_kscale(k):
    if not WIDE:
        return np.ones(k)
    levels = np.array([10, -10, 5, -5, 0])
    a = np.random.permutation(np.resize(levels, k // 512 * 4)).reshape(k // 512, 4)
    idx = np.arange(k)
    return np.exp2(a[idx // 512, idx % 128 // 32])


BF16 = ml_dtypes.bfloat16


def bf(x):
    return np.asarray(x, np.float32).astype(BF16)


def f64(x):
    return np.asarray(x).astype(np.float64)


B, S, D, H, DN, DR, DV, RQ, RKV = 4, 1024, 512, 4, 128, 128, 128, 1536, 512
THETA = 10000.0
EPS = 1e-6


def rmsnorm(v, w):
    return v * (1.0 / np.sqrt(np.mean(v * v, axis=-1, keepdims=True) + EPS)) * w


def rotate_half(v):
    v1 = v[..., ::2]
    v2 = v[..., 1::2]
    return np.stack((-v2, v1), axis=-1).reshape(v.shape)


def rope_cache():
    inv_freq = 1.0 / THETA ** (np.arange(0, DR, 2) / DR)
    freqs = np.outer(np.arange(S), inv_freq)
    emb = np.concatenate((freqs, freqs), -1)
    return np.cos(emb), np.sin(emb)


def apply_rope(v, cos, sin):
    return v * cos[None, None] + rotate_half(v) * sin[None, None]


def setup_inputs():
    s, t = mx_kscale(D), mx_kscale(RKV)
    return {"x": bf(np.random.standard_normal((B, S, D)) * s),
            "Wkva": bf(np.random.standard_normal((D, RKV + DR)) / np.sqrt(D) / s[:, None]),
            "kv_a_norm_w": bf((1.0 + 0.1 * np.random.standard_normal(RKV)) * t),
            "Wkvb": bf(np.random.standard_normal((RKV, H * (DN + DV))) / np.sqrt(RKV) / t[:, None])}


def reference(x, Wkva, kv_a_norm_w, Wkvb):
    kv_a = mxq(f64(x), 2, "e4m3") @ mxq(f64(Wkva), 0, "e4m3")
    kv_latent, k_rope_shared = kv_a[..., :RKV], kv_a[..., RKV:]
    h = rmsnorm(kv_latent, f64(kv_a_norm_w))
    kv = mxq(h, 2, "e4m3") @ mxq(f64(Wkvb), 0, "e4m3")
    kv = kv.reshape(B, S, H, DN + DV).transpose(0, 2, 1, 3)
    k_nope, v = kv[..., :DN], kv[..., DN:]
    cos, sin = rope_cache()
    k_rope = apply_rope(k_rope_shared[:, None], cos, sin)
    k_rope = np.broadcast_to(k_rope, (B, H, S, DR))
    k_final = np.concatenate([k_nope, k_rope], -1)
    return k_final, v

@@ -1,0 +1,281 @@
+import math
+from contextlib import ExitStack
+
+import concourse.mybir as mybir
+from concourse.masks import make_identity
+
+F32 = mybir.dt.float32
+BF16 = mybir.dt.bfloat16
+I32 = mybir.dt.int32
+U32 = mybir.dt.uint32
+U8 = mybir.dt.uint8
+FP8X4 = mybir.dt.float8_e4m3fn_x4
+ALU = mybir.AluOpType
+ACT = mybir.ActivationFunctionType
+
+P = 128
+PACK = 4
+BATCH, SEQ, D_MODEL, HEADS = 4, 1024, 512, 4
+D_NOPE, D_ROPE, D_V, R_KV = 128, 128, 128, 512
+ROPE_BASE = 10000.0
+EPS = 1e-6
+
+TOKENS = BATCH * SEQ
+N_TILES = TOKENS // P
+TILES_PER_GROUP = 4
+GROUP = P * TILES_PER_GROUP
+N_GROUPS = TOKENS // GROUP
+GROUPS_PER_SEQ = SEQ // GROUP
+TILES_PER_STORE = 2
+N_POS = GROUPS_PER_SEQ * TILES_PER_GROUP
+N_FREQ = D_ROPE // 2
+ROUND_MAGIC = 1.5 * 2.0**23
+
+FLOPS = 2 * TOKENS * D_MODEL * (R_KV + D_ROPE) + 2 * TOKENS * R_KV * HEADS * (D_NOPE + D_V)
+
+
+def tile_multiheadlatentattention_pb_t_kernel(tc, x, Wkva, kv_a_norm_w, Wkvb, out_0, out_1):
+    nc = tc.nc
+    x_groups = x.flatten_outer_dims().rearrange("(g p i) k -> g p (i k)", p=P, i=TILES_PER_GROUP)
+    k_groups = out_0.rearrange("b h (g p i) d -> b g p h (i d)", p=P, i=TILES_PER_GROUP)
+    v_groups = out_1.rearrange("b h (g p i) d -> b g p h (i d)", p=P, i=TILES_PER_GROUP)
+
+    with ExitStack() as ctx:
+        ctx.enter_context(tc.manual_schedule())
+        consts = ctx.enter_context(tc.tile_pool(name="consts", bufs=1))
+        x_pool = ctx.enter_context(tc.tile_pool(name="x_pool", bufs=1))
+        work = ctx.enter_context(tc.tile_pool(name="work", bufs=4))
+        small = ctx.enter_context(tc.tile_pool(name="small", bufs=8))
+        psum_xt = ctx.enter_context(tc.psum_pool(name="psum_xt", bufs=1))
+        psum_c = ctx.enter_context(tc.psum_pool(name="psum_c", bufs=2))
+        psum_r = ctx.enter_context(tc.psum_pool(name="psum_r", bufs=1))
+        psum_ht = ctx.enter_context(tc.psum_pool(name="psum_ht", bufs=1))
+        psum_kv = ctx.enter_context(tc.psum_pool(name="psum_kv", bufs=3))
+
+        wa_raw = consts.tile([P, PACK, R_KV + D_ROPE], BF16)
+        nc.sync.dma_start(
+            out=wa_raw[:].rearrange("q (u e) c -> q u (e c)", u=2),
+            in_=Wkva.rearrange("(u q e) c -> q u (e c)", u=2, e=2),
+        )
+        x_sb = []
+        for g in range(N_GROUPS):
+            x_tile = x_pool.tile([P, TILES_PER_GROUP * D_MODEL], BF16, name="x_sb%d" % g)
+            x_sb.append(x_tile)
+        nc.sync.dma_start(out=x_sb[0][:], in_=x_groups[0])
+        gain_bc = consts.tile([P, R_KV], BF16)
+        nc.scalar.dma_start(out=gain_bc[:], in_=kv_a_norm_w.partition_broadcast(P))
+        wb_raw = consts.tile([P, PACK, HEADS * (D_NOPE + D_V)], BF16)
+        nc.sync.dma_start(out=wb_raw[:], in_=Wkvb.rearrange("(t p) n -> p t n", p=P))
+        for g in range(1, N_GROUPS):
+            nc.sync.dma_start(out=x_sb[g][:], in_=x_groups[g])
+
+        pos_i = consts.tile([P, N_POS], I32)
+        nc.gpsimd.iota(pos_i[:], pattern=[[GROUP, GROUPS_PER_SEQ], [1, TILES_PER_GROUP]], base=0,
+                       channel_multiplier=TILES_PER_GROUP)
+        ident_f32 = consts.tile([P, P], F32)
+        make_identity(nc, ident_f32[:])
+        ident_bf16 = consts.tile([P, P], BF16)
+        make_identity(nc, ident_bf16[:])
+        eps_col = consts.tile([P, 1], F32)
+        nc.vector.memset(eps_col[:], EPS)
+
+        cos_sin = consts.tile([P, N_POS, 2 * D_ROPE], F32)
+        trig = ctx.enter_context(tc.tile_pool(name="trig", bufs=1))
+        shape = [P, N_POS, N_FREQ]
+        twice = [P, N_POS, 2, N_FREQ]
+        pos = trig.tile([P, N_POS], F32)
+        nc.vector.tensor_copy(out=pos[:], in_=pos_i[:])
+        freq = trig.tile([P, N_FREQ], F32)
+        nc.vector.memset(freq[:, 0:1], 1.0)
+        for doubling in range(6):
+            have = 2**doubling
+            nc.vector.tensor_scalar(out=freq[:, have:2 * have], in0=freq[:, 0:have],
+                                    scalar1=ROPE_BASE ** (-have / N_FREQ), scalar2=None, op0=ALU.mult)
+        turns = trig.tile(shape, F32)
+        nc.vector.scalar_tensor_tensor(out=turns[:], in0=freq[:].unsqueeze(1).to_broadcast(shape),
+                                       scalar=0.5 / math.pi, in1=pos[:].unsqueeze(2).to_broadcast(shape),
+                                       op0=ALU.mult, op1=ALU.mult)
+        whole = trig.tile(shape, F32)
+        nc.vector.tensor_scalar(out=whole[:], in0=turns[:], scalar1=ROUND_MAGIC, scalar2=ROUND_MAGIC,
+                                op0=ALU.add, op1=ALU.subtract)
+        frac = trig.tile(shape, F32)
+        nc.vector.tensor_tensor(out=frac[:], in0=turns[:], in1=whole[:], op=ALU.subtract)
+        sin_quarter = trig.tile(shape, F32)
+        nc.scalar.activation(out=sin_quarter[:], in_=frac[:], func=ACT.Sin, scale=0.5 * math.pi)
+        sin_half = trig.tile(shape, F32)
+        nc.scalar.activation(out=sin_half[:], in_=frac[:], func=ACT.Sin, scale=math.pi)
+        sq_quarter = trig.tile(shape, F32)
+        nc.scalar.activation(out=sq_quarter[:], in_=sin_quarter[:], func=ACT.Square)
+        two_cos_half = trig.tile(shape, F32)
+        nc.scalar.activation(out=two_cos_half[:], in_=sq_quarter[:], func=ACT.Copy, bias=2.0, scale=-4.0)
+        sq_half = trig.tile(shape, F32)
+        nc.scalar.activation(out=sq_half[:], in_=sin_half[:], func=ACT.Square)
+        nc.scalar.activation(out=cos_sin[:, :, 0:D_ROPE].rearrange("p s (r j) -> p s r j", r=2),
+                             in_=sq_half[:].unsqueeze(2).to_broadcast(twice), func=ACT.Copy, bias=1.0, scale=-2.0)
+
+        wa_cols = R_KV + 2 * D_ROPE
+        wa_grouped = consts.tile([P, wa_cols, PACK], BF16, align_bytes=64)
+        wa_codes = consts.tile([P, wa_cols], U32, align_bytes=64)
+        wa_scales = consts.tile([P, wa_cols], U8, align_bytes=64)
+        nc.vector.tensor_copy(out=wa_grouped[:, 0:R_KV, :], in_=wa_raw[:, :, 0:R_KV].rearrange("p t c -> p c t"))
+        nc.vector.quantize_mx(out=wa_codes[:, 0:R_KV].bitcast(FP8X4), scales=wa_scales[:, 0:R_KV],
+                              in_=wa_grouped[:, 0:R_KV, :].rearrange("p c t -> p (c t)"))
+        rope_raw = wa_raw[:, :, R_KV:R_KV + D_ROPE]
+        raw_pairs = rope_raw.rearrange("p t (i two) -> p i two t", two=2)
+        rot_pairs = wa_grouped[:, R_KV + D_ROPE:wa_cols, :].rearrange("p (i two) t -> p i two t", two=2)
+        nc.gpsimd.tensor_scalar(out=wa_grouped[:, R_KV:R_KV + D_ROPE, :], in0=rope_raw.rearrange("p t c -> p c t"),
+                                scalar1=1.0, scalar2=0.0, op0=ALU.mult, op1=ALU.add)
+        nc.gpsimd.tensor_scalar(out=rot_pairs[:, :, 0, :], in0=raw_pairs[:, :, 1, :], scalar1=-1.0, scalar2=0.0,
+                                op0=ALU.mult, op1=ALU.add)
+        nc.gpsimd.tensor_scalar(out=rot_pairs[:, :, 1, :], in0=raw_pairs[:, :, 0, :], scalar1=1.0, scalar2=0.0,
+                                op0=ALU.mult, op1=ALU.add)
+        nc.gpsimd.tensor_tensor(out=cos_sin[:, :, D_ROPE:2 * D_ROPE].rearrange("p s (r j) -> p s r j", r=2),
+                                in0=sin_half[:].unsqueeze(2).to_broadcast(twice),
+                                in1=two_cos_half[:].unsqueeze(2).to_broadcast(twice), op=ALU.mult)
+
+        wb_cols = HEADS * (D_NOPE + D_V)
+        half_cols = wb_cols // 2
+        wb_grouped = consts.tile([P, wb_cols, PACK], BF16, align_bytes=64)
+        wb_codes = consts.tile([P, wb_cols], U32, align_bytes=64)
+        wb_scales = consts.tile([P, wb_cols], U8, align_bytes=64)
+        wb_parts = wb_raw[:].rearrange("p t (h kv d) -> p kv h d t", kv=2, d=D_NOPE)
+        for kv in range(2):
+            cols = slice(kv * half_cols, (kv + 1) * half_cols)
+            nc.gpsimd.tensor_scalar(out=wb_grouped[:, cols, :].rearrange("p (h d) t -> p h d t", h=HEADS),
+                                    in0=wb_parts[:, kv], scalar1=1.0, scalar2=0.0, op0=ALU.mult, op1=ALU.add)
+
+        def quantise_wa_rope():
+            nc.vector.quantize_mx(out=wa_codes[:, R_KV:wa_cols].bitcast(FP8X4), scales=wa_scales[:, R_KV:wa_cols],
+                                  in_=wa_grouped[:, R_KV:wa_cols, :].rearrange("p c t -> p (c t)"))
+
+        def quantise_wb(kv):
+            cols = slice(kv * half_cols, (kv + 1) * half_cols)
+            nc.vector.quantize_mx(out=wb_codes[:, cols].bitcast(FP8X4), scales=wb_scales[:, cols],
+                                  in_=wb_grouped[:, cols, :].rearrange("p c t -> p (c t)"))
+
+        outs = ctx.enter_context(tc.tile_pool(name="outs", bufs=6))
+        xt_ps, xg_sb, xq, c_ps, r_ps, h_sb, ht_ps, hg_sb, hq, k_sb, v_sb = {}, {}, {}, {}, {}, {}, {}, {}, {}, {}, {}
+
+        def transpose_x(n):
+            g, i = divmod(n, TILES_PER_GROUP)
+            words = x_sb[g][:].bitcast(F32)
+            xt_ps[n] = psum_xt.tile([P, 2, P], F32, name="xt_ps")
+            for u in range(2):
+                first = (i * 2 + u) * P
+                nc.tensor.transpose(xt_ps[n][:, u, :], words[:, first:first + P], ident_f32[:])
+
+        def group_x(n):
+            xg_sb[n] = work.tile([P, P * PACK], BF16, name="xg_sb", align_bytes=64)
+            dst = xg_sb[n][:].bitcast(F32).rearrange("p (n u) -> p n u", u=2)
+            src = xt_ps[n][:].rearrange("p u n -> p n u")
+            if n % 2 == 0:
+                nc.vector.tensor_copy(out=dst, in_=src)
+            else:
+                nc.scalar.copy(out=dst, in_=src)
+
+        def quantise_x(n):
+            codes = work.tile([P, P], U32, name="xq_codes", align_bytes=64)
+            scales = work.tile([P, P], U8, name="xq_scales", align_bytes=64)
+            nc.vector.quantize_mx(out=codes[:].bitcast(FP8X4), scales=scales[:], in_=xg_sb[n][:])
+            xq[n] = (codes, scales)
+
+        def first_product(n):
+            codes, scales = xq[n]
+            c_ps[n] = psum_c.tile([P, R_KV], F32, name="c_ps")
+            nc.tensor.matmul_mx(out=c_ps[n][:], lhsT=codes[:].bitcast(FP8X4), lhsT_scale=scales[:],
+                                rhs=wa_codes[:, 0:R_KV].bitcast(FP8X4), rhs_scale=wa_scales[:, 0:R_KV],
+                                start=True, stop=True)
+            r_ps[n] = psum_r.tile([P, 2 * D_ROPE], F32, name="r_ps")
+            nc.tensor.matmul_mx(out=r_ps[n][:], lhsT=codes[:].bitcast(FP8X4), lhsT_scale=scales[:],
+                                rhs=wa_codes[:, R_KV:wa_cols].bitcast(FP8X4), rhs_scale=wa_scales[:, R_KV:wa_cols],
+                                start=True, stop=True)
+
+        def normalise(n):
+            squares = work.tile([P, R_KV], BF16, name="squares")
+            sum_sq = small.tile([P, 1], F32, name="sum_sq")
+            nc.scalar.activation(out=squares[:], in_=c_ps[n][:], func=ACT.Square, accum_out=sum_sq[:])
+            rms = small.tile([P, 1], F32, name="rms")
+            nc.scalar.activation(out=rms[:], in_=sum_sq[:], func=ACT.Sqrt, bias=eps_col[:], scale=1.0 / R_KV)
+            inv_rms = small.tile([P, 1], F32, name="inv_rms")
+            nc.vector.reciprocal(out=inv_rms[:], in_=rms[:])
+            h_sb[n] = work.tile([P, R_KV], BF16, name="h_sb")
+            nc.vector.scalar_tensor_tensor(out=h_sb[n][:], in0=c_ps[n][:], scalar=inv_rms[:], in1=gain_bc[:],
+                                           op0=ALU.mult, op1=ALU.mult)
+
+        def rotate(n):
+            unit, j = divmod(n, TILES_PER_STORE)
+            if j == 0:
+                k_sb[unit] = outs.tile([P, HEADS, TILES_PER_STORE, D_NOPE + D_ROPE], F32, name="k_sb")
+                v_sb[unit] = outs.tile([P, HEADS, TILES_PER_STORE, D_V], F32, name="v_sb")
+            prod = work.tile([P, 2, D_ROPE], F32, name="prod")
+            nc.vector.tensor_tensor(out=prod[:].rearrange("p c d -> p (c d)"), in0=r_ps[n][:],
+                                    in1=cos_sin[:, n % N_POS, :], op=ALU.mult)
+            spread = [P, HEADS, D_ROPE]
+            nc.gpsimd.tensor_tensor(out=k_sb[unit][:, :, j, D_NOPE:D_NOPE + D_ROPE],
+                                    in0=prod[:, 0, :].unsqueeze(1).to_broadcast(spread),
+                                    in1=prod[:, 1, :].unsqueeze(1).to_broadcast(spread), op=ALU.add)
+
+        def transpose_h(n):
+            ht_ps[n] = psum_ht.tile([P, PACK, P], BF16, name="ht_ps")
+            for t in range(PACK):
+                nc.tensor.transpose(ht_ps[n][:, t, :], h_sb[n][:, t * P:(t + 1) * P], ident_bf16[:])
+
+        def group_h(n):
+            hg_sb[n] = work.tile([P, P, PACK], BF16, name="hg_sb", align_bytes=64)
+            nc.vector.tensor_copy(out=hg_sb[n][:], in_=ht_ps[n][:].rearrange("p t n -> p n t"))
+
+        def quantise_h(n):
+            codes = work.tile([P, P], U32, name="hq_codes", align_bytes=64)
+            scales = work.tile([P, P], U8, name="hq_scales", align_bytes=64)
+            nc.vector.quantize_mx(out=codes[:].bitcast(FP8X4), scales=scales[:],
+                                  in_=hg_sb[n][:].rearrange("p n t -> p (n t)"))
+            hq[n] = (codes, scales)
+
+        def second_product(n):
+            unit, j = divmod(n, TILES_PER_STORE)
+            codes, scales = hq[n]
+            for kv in range(2):
+                cols = slice(kv * half_cols, (kv + 1) * half_cols)
+                kv_ps = psum_kv.tile([P, half_cols], F32, name="kv_ps")
+                nc.tensor.matmul_mx(out=kv_ps[:], lhsT=codes[:].bitcast(FP8X4), lhsT_scale=scales[:],
+                                    rhs=wb_codes[:, cols].bitcast(FP8X4), rhs_scale=wb_scales[:, cols],
+                                    start=True, stop=True)
+                dst = k_sb[unit][:, :, j, 0:D_NOPE] if kv == 0 else v_sb[unit][:, :, j, :]
+                nc.scalar.copy(out=dst, in_=kv_ps[:].rearrange("p (h d) -> p h d", h=HEADS))
+            if j == TILES_PER_STORE - 1:
+                g, last = divmod(n, TILES_PER_GROUP)
+                b, gs = divmod(g, GROUPS_PER_SEQ)
+                i0 = last + 1 - TILES_PER_STORE
+                k_w, v_w = D_NOPE + D_ROPE, D_V
+                nc.sync.dma_start(out=k_groups[b, gs][:, :, i0 * k_w:(last + 1) * k_w],
+                                  in_=k_sb[unit][:].rearrange("p h i d -> p h (i d)"))
+                nc.sync.dma_start(out=v_groups[b, gs][:, :, i0 * v_w:(last + 1) * v_w],
+                                  in_=v_sb[unit][:].rearrange("p h i d -> p h (i d)"))
+
+        def live(n):
+            return 0 <= n < N_TILES
+
+        for step in range(-1, N_TILES + 3):
+            ahead, now, again, leaving = step + 1, step, step - 2, step - 3
+            if live(ahead):
+                transpose_x(ahead)
+            if live(again):
+                transpose_h(again)
+            if live(ahead):
+                group_x(ahead)
+            if live(again):
+                group_h(again)
+            if live(ahead):
+                quantise_x(ahead)
+            if live(again):
+                quantise_h(again)
+            if ahead == 0:
+                quantise_wa_rope()
+            if again in (0, 1):
+                quantise_wb(again)
+            if live(now):
+                first_product(now)
+                normalise(now)
+                rotate(now)
+            if live(leaving):
+                second_product(leaving)

@@ -48,9 +48,9 @@ def tile_multiheadlatentattention_pb_t_kernel(tc, x, Wkva, kv_a_norm_w, Wkvb, ou
         small = ctx.enter_context(tc.tile_pool(name="small", bufs=8))
         psum_xt = ctx.enter_context(tc.psum_pool(name="psum_xt", bufs=1))
         psum_c = ctx.enter_context(tc.psum_pool(name="psum_c", bufs=2))
-        psum_r = ctx.enter_context(tc.psum_pool(name="psum_r", bufs=1))
+        psum_r = ctx.enter_context(tc.psum_pool(name="psum_r", bufs=2))
         psum_ht = ctx.enter_context(tc.psum_pool(name="psum_ht", bufs=1))
-        psum_kv = ctx.enter_context(tc.psum_pool(name="psum_kv", bufs=3))
+        psum_kv = ctx.enter_context(tc.psum_pool(name="psum_kv", bufs=2))
 
         wa_raw = consts.tile([P, PACK, R_KV + D_ROPE], BF16)
         nc.sync.dma_start(
@@ -179,12 +179,15 @@ def tile_multiheadlatentattention_pb_t_kernel(tc, x, Wkva, kv_a_norm_w, Wkvb, ou
             nc.vector.quantize_mx(out=codes[:].bitcast(FP8X4), scales=scales[:], in_=xg_sb[n][:])
             xq[n] = (codes, scales)
 
-        def first_product(n):
+        def latent_product(n):
             codes, scales = xq[n]
             c_ps[n] = psum_c.tile([P, R_KV], F32, name="c_ps")
             nc.tensor.matmul_mx(out=c_ps[n][:], lhsT=codes[:].bitcast(FP8X4), lhsT_scale=scales[:],
                                 rhs=wa_codes[:, 0:R_KV].bitcast(FP8X4), rhs_scale=wa_scales[:, 0:R_KV],
                                 start=True, stop=True)
+
+        def rope_product(n):
+            codes, scales = xq[n]
             r_ps[n] = psum_r.tile([P, 2 * D_ROPE], F32, name="r_ps")
             nc.tensor.matmul_mx(out=r_ps[n][:], lhsT=codes[:].bitcast(FP8X4), lhsT_scale=scales[:],
                                 rhs=wa_codes[:, R_KV:wa_cols].bitcast(FP8X4), rhs_scale=wa_scales[:, R_KV:wa_cols],
@@ -273,9 +276,12 @@ def tile_multiheadlatentattention_pb_t_kernel(tc, x, Wkva, kv_a_norm_w, Wkvb, ou
                 quantise_wa_rope()
             if again in (0, 1):
                 quantise_wb(again)
+            if live(now - 1):
+                rotate(now - 1)
             if live(now):
-                first_product(now)
+                latent_product(now)
                 normalise(now)
-                rotate(now)
             if live(leaving):
                 second_product(leaving)
+            if live(now):
+                rope_product(now)

@@ -44,8 +44,10 @@ def tile_multiheadlatentattention_pb_t_kernel(tc, x, Wkva, kv_a_norm_w, Wkvb, ou
         ctx.enter_context(tc.manual_schedule())
         consts = ctx.enter_context(tc.tile_pool(name="consts", bufs=1))
         x_pool = ctx.enter_context(tc.tile_pool(name="x_pool", bufs=1))
+        trig = ctx.enter_context(tc.tile_pool(name="trig", bufs=1))
         work = ctx.enter_context(tc.tile_pool(name="work", bufs=4))
         small = ctx.enter_context(tc.tile_pool(name="small", bufs=8))
+        outs = ctx.enter_context(tc.tile_pool(name="outs", bufs=6))
         psum_xt = ctx.enter_context(tc.psum_pool(name="psum_xt", bufs=1))
         psum_c = ctx.enter_context(tc.psum_pool(name="psum_c", bufs=2))
         psum_r = ctx.enter_context(tc.psum_pool(name="psum_r", bufs=2))
@@ -79,10 +81,7 @@ def tile_multiheadlatentattention_pb_t_kernel(tc, x, Wkva, kv_a_norm_w, Wkvb, ou
         eps_col = consts.tile([P, 1], F32)
         nc.vector.memset(eps_col[:], EPS)
 
-        cos_sin = consts.tile([P, N_POS, 2 * D_ROPE], F32)
-        trig = ctx.enter_context(tc.tile_pool(name="trig", bufs=1))
         shape = [P, N_POS, N_FREQ]
-        twice = [P, N_POS, 2, N_FREQ]
         pos = trig.tile([P, N_POS], F32)
         nc.vector.tensor_copy(out=pos[:], in_=pos_i[:])
         freq = trig.tile([P, N_FREQ], F32)
@@ -98,20 +97,16 @@ def tile_multiheadlatentattention_pb_t_kernel(tc, x, Wkva, kv_a_norm_w, Wkvb, ou
         whole = trig.tile(shape, F32)
         nc.vector.tensor_scalar(out=whole[:], in0=turns[:], scalar1=ROUND_MAGIC, scalar2=ROUND_MAGIC,
                                 op0=ALU.add, op1=ALU.subtract)
-        frac = trig.tile(shape, F32)
-        nc.vector.tensor_tensor(out=frac[:], in0=turns[:], in1=whole[:], op=ALU.subtract)
-        sin_quarter = trig.tile(shape, F32)
-        nc.scalar.activation(out=sin_quarter[:], in_=frac[:], func=ACT.Sin, scale=0.5 * math.pi)
-        sin_half = trig.tile(shape, F32)
-        nc.scalar.activation(out=sin_half[:], in_=frac[:], func=ACT.Sin, scale=math.pi)
-        sq_quarter = trig.tile(shape, F32)
-        nc.scalar.activation(out=sq_quarter[:], in_=sin_quarter[:], func=ACT.Square)
-        two_cos_half = trig.tile(shape, F32)
-        nc.scalar.activation(out=two_cos_half[:], in_=sq_quarter[:], func=ACT.Copy, bias=2.0, scale=-4.0)
-        sq_half = trig.tile(shape, F32)
-        nc.scalar.activation(out=sq_half[:], in_=sin_half[:], func=ACT.Square)
-        nc.scalar.activation(out=cos_sin[:, :, 0:D_ROPE].rearrange("p s (r j) -> p s r j", r=2),
-                             in_=sq_half[:].unsqueeze(2).to_broadcast(twice), func=ACT.Copy, bias=1.0, scale=-2.0)
+        part = trig.tile([P, 2, N_POS, N_FREQ], F32)
+        nc.vector.tensor_tensor(out=part[:, 0], in0=turns[:], in1=whole[:], op=ALU.subtract)
+        nc.vector.tensor_scalar(out=part[:, 1], in0=part[:, 0], scalar1=0.25, scalar2=None, op0=ALU.subtract)
+        half_sin = trig.tile([P, 2, N_POS, N_FREQ], F32)
+        nc.scalar.activation(out=half_sin[:], in_=part[:], func=ACT.Sin, scale=math.pi)
+        half_sq = trig.tile([P, 2, N_POS, N_FREQ], F32)
+        nc.scalar.activation(out=half_sq[:], in_=half_sin[:], func=ACT.Square)
+        cos_sin = consts.tile([P, N_POS, 2, N_FREQ], F32)
+        nc.scalar.activation(out=cos_sin[:], in_=half_sq[:].rearrange("p c s j -> p s c j"), func=ACT.Copy,
+                             bias=1.0, scale=-2.0)
 
         wa_cols = R_KV + 2 * D_ROPE
         wa_grouped = consts.tile([P, wa_cols, PACK], BF16, align_bytes=64)
@@ -129,9 +124,10 @@ def tile_multiheadlatentattention_pb_t_kernel(tc, x, Wkva, kv_a_norm_w, Wkvb, ou
                                 op0=ALU.mult, op1=ALU.add)
         nc.gpsimd.tensor_scalar(out=rot_pairs[:, :, 1, :], in0=raw_pairs[:, :, 0, :], scalar1=1.0, scalar2=0.0,
                                 op0=ALU.mult, op1=ALU.add)
-        nc.gpsimd.tensor_tensor(out=cos_sin[:, :, D_ROPE:2 * D_ROPE].rearrange("p s (r j) -> p s r j", r=2),
-                                in0=sin_half[:].unsqueeze(2).to_broadcast(twice),
-                                in1=two_cos_half[:].unsqueeze(2).to_broadcast(twice), op=ALU.mult)
+
+        def quantise_wa_rope():
+            nc.vector.quantize_mx(out=wa_codes[:, R_KV:wa_cols].bitcast(FP8X4), scales=wa_scales[:, R_KV:wa_cols],
+                                  in_=wa_grouped[:, R_KV:wa_cols, :].rearrange("p c t -> p (c t)"))
 
         wb_cols = HEADS * (D_NOPE + D_V)
         half_cols = wb_cols // 2
@@ -139,22 +135,24 @@ def tile_multiheadlatentattention_pb_t_kernel(tc, x, Wkva, kv_a_norm_w, Wkvb, ou
         wb_codes = consts.tile([P, wb_cols], U32, align_bytes=64)
         wb_scales = consts.tile([P, wb_cols], U8, align_bytes=64)
         wb_parts = wb_raw[:].rearrange("p t (h kv d) -> p kv h d t", kv=2, d=D_NOPE)
-        for kv in range(2):
-            cols = slice(kv * half_cols, (kv + 1) * half_cols)
-            nc.gpsimd.tensor_scalar(out=wb_grouped[:, cols, :].rearrange("p (h d) t -> p h d t", h=HEADS),
-                                    in0=wb_parts[:, kv], scalar1=1.0, scalar2=0.0, op0=ALU.mult, op1=ALU.add)
 
-        def quantise_wa_rope():
-            nc.vector.quantize_mx(out=wa_codes[:, R_KV:wa_cols].bitcast(FP8X4), scales=wa_scales[:, R_KV:wa_cols],
-                                  in_=wa_grouped[:, R_KV:wa_cols, :].rearrange("p c t -> p (c t)"))
+        def group_wb(kv):
+            cols = slice(kv * half_cols, (kv + 1) * half_cols)
+            dst = wb_grouped[:, cols, :].rearrange("p (h d) t -> p h d t", h=HEADS)
+            if kv == 0:
+                nc.vector.tensor_copy(out=dst, in_=wb_parts[:, kv])
+            else:
+                nc.scalar.copy(out=dst, in_=wb_parts[:, kv])
 
         def quantise_wb(kv):
             cols = slice(kv * half_cols, (kv + 1) * half_cols)
             nc.vector.quantize_mx(out=wb_codes[:, cols].bitcast(FP8X4), scales=wb_scales[:, cols],
                                   in_=wb_grouped[:, cols, :].rearrange("p c t -> p (c t)"))
 
-        outs = ctx.enter_context(tc.tile_pool(name="outs", bufs=6))
-        xt_ps, xg_sb, xq, c_ps, r_ps, h_sb, ht_ps, hg_sb, hq, k_sb, v_sb = {}, {}, {}, {}, {}, {}, {}, {}, {}, {}, {}
+        xt_ps, c_ps, r_ps, inv_rms, h_sb, ht_ps, grouped, xq, hq, k_sb, v_sb = {}, {}, {}, {}, {}, {}, {}, {}, {}, {}, {}
+
+        def live(n):
+            return 0 <= n < N_TILES
 
         def transpose_x(n):
             g, i = divmod(n, TILES_PER_GROUP)
@@ -164,45 +162,59 @@ def tile_multiheadlatentattention_pb_t_kernel(tc, x, Wkva, kv_a_norm_w, Wkvb, ou
                 first = (i * 2 + u) * P
                 nc.tensor.transpose(xt_ps[n][:, u, :], words[:, first:first + P], ident_f32[:])
 
-        def group_x(n):
-            xg_sb[n] = work.tile([P, P * PACK], BF16, name="xg_sb", align_bytes=64)
-            dst = xg_sb[n][:].bitcast(F32).rearrange("p (n u) -> p n u", u=2)
-            src = xt_ps[n][:].rearrange("p u n -> p n u")
-            if n % 2 == 0:
-                nc.vector.tensor_copy(out=dst, in_=src)
-            else:
-                nc.scalar.copy(out=dst, in_=src)
+        def transpose_h(n):
+            ht_ps[n] = psum_ht.tile([P, PACK, P], BF16, name="ht_ps")
+            for t in range(PACK):
+                nc.tensor.transpose(ht_ps[n][:, t, :], h_sb[n][:, t * P:(t + 1) * P], ident_bf16[:])
 
-        def quantise_x(n):
-            codes = work.tile([P, P], U32, name="xq_codes", align_bytes=64)
-            scales = work.tile([P, P], U8, name="xq_scales", align_bytes=64)
-            nc.vector.quantize_mx(out=codes[:].bitcast(FP8X4), scales=scales[:], in_=xg_sb[n][:])
-            xq[n] = (codes, scales)
+        def group_both(step, nx, nh):
+            grouped[step] = work.tile([P, 2 * P * PACK], BF16, name="grouped", align_bytes=64)
+            if live(nx):
+                dst = grouped[step][:].bitcast(F32)[:, 0:2 * P].rearrange("p (n u) -> p n u", u=2)
+                src = xt_ps[nx][:].rearrange("p u n -> p n u")
+                if nx % 2 == 0:
+                    nc.vector.tensor_copy(out=dst, in_=src)
+                else:
+                    nc.scalar.copy(out=dst, in_=src)
+            if live(nh):
+                nc.vector.tensor_copy(out=grouped[step][:, P * PACK:].rearrange("p (n t) -> p n t", t=PACK),
+                                      in_=ht_ps[nh][:].rearrange("p t n -> p n t"))
+
+        def quantise_both(step, nx, nh):
+            codes = work.tile([P, 2 * P], U32, name="codes", align_bytes=64)
+            scales = work.tile([P, 2 * P], U8, name="scales", align_bytes=64)
+            lo = 0 if live(nx) else P
+            hi = 2 * P if live(nh) else P
+            nc.vector.quantize_mx(out=codes[:, lo:hi].bitcast(FP8X4), scales=scales[:, lo:hi],
+                                  in_=grouped[step][:, lo * PACK:hi * PACK])
+            xq[nx] = (codes[:, 0:P], scales[:, 0:P])
+            hq[nh] = (codes[:, P:2 * P], scales[:, P:2 * P])
 
         def latent_product(n):
             codes, scales = xq[n]
             c_ps[n] = psum_c.tile([P, R_KV], F32, name="c_ps")
-            nc.tensor.matmul_mx(out=c_ps[n][:], lhsT=codes[:].bitcast(FP8X4), lhsT_scale=scales[:],
+            nc.tensor.matmul_mx(out=c_ps[n][:], lhsT=codes.bitcast(FP8X4), lhsT_scale=scales,
                                 rhs=wa_codes[:, 0:R_KV].bitcast(FP8X4), rhs_scale=wa_scales[:, 0:R_KV],
                                 start=True, stop=True)
 
         def rope_product(n):
             codes, scales = xq[n]
             r_ps[n] = psum_r.tile([P, 2 * D_ROPE], F32, name="r_ps")
-            nc.tensor.matmul_mx(out=r_ps[n][:], lhsT=codes[:].bitcast(FP8X4), lhsT_scale=scales[:],
+            nc.tensor.matmul_mx(out=r_ps[n][:], lhsT=codes.bitcast(FP8X4), lhsT_scale=scales,
                                 rhs=wa_codes[:, R_KV:wa_cols].bitcast(FP8X4), rhs_scale=wa_scales[:, R_KV:wa_cols],
                                 start=True, stop=True)
 
-        def normalise(n):
+        def measure(n):
             squares = work.tile([P, R_KV], BF16, name="squares")
             sum_sq = small.tile([P, 1], F32, name="sum_sq")
             nc.scalar.activation(out=squares[:], in_=c_ps[n][:], func=ACT.Square, accum_out=sum_sq[:])
-            rms = small.tile([P, 1], F32, name="rms")
-            nc.scalar.activation(out=rms[:], in_=sum_sq[:], func=ACT.Sqrt, bias=eps_col[:], scale=1.0 / R_KV)
-            inv_rms = small.tile([P, 1], F32, name="inv_rms")
-            nc.vector.reciprocal(out=inv_rms[:], in_=rms[:])
+            inv_rms[n] = small.tile([P, 1], F32, name="inv_rms")
+            nc.scalar.activation(out=inv_rms[n][:], in_=sum_sq[:], func=ACT.Abs_reciprocal_sqrt, bias=eps_col[:],
+                                 scale=1.0 / R_KV)
+
+        def normalise(n):
             h_sb[n] = work.tile([P, R_KV], BF16, name="h_sb")
-            nc.vector.scalar_tensor_tensor(out=h_sb[n][:], in0=c_ps[n][:], scalar=inv_rms[:], in1=gain_bc[:],
+            nc.vector.scalar_tensor_tensor(out=h_sb[n][:], in0=c_ps[n][:], scalar=inv_rms[n][:], in1=gain_bc[:],
                                            op0=ALU.mult, op1=ALU.mult)
 
         def rotate(n):
@@ -210,29 +222,16 @@ def tile_multiheadlatentattention_pb_t_kernel(tc, x, Wkva, kv_a_norm_w, Wkvb, ou
             if j == 0:
                 k_sb[unit] = outs.tile([P, HEADS, TILES_PER_STORE, D_NOPE + D_ROPE], F32, name="k_sb")
                 v_sb[unit] = outs.tile([P, HEADS, TILES_PER_STORE, D_V], F32, name="v_sb")
-            prod = work.tile([P, 2, D_ROPE], F32, name="prod")
-            nc.vector.tensor_tensor(out=prod[:].rearrange("p c d -> p (c d)"), in0=r_ps[n][:],
-                                    in1=cos_sin[:, n % N_POS, :], op=ALU.mult)
-            spread = [P, HEADS, D_ROPE]
-            nc.gpsimd.tensor_tensor(out=k_sb[unit][:, :, j, D_NOPE:D_NOPE + D_ROPE],
-                                    in0=prod[:, 0, :].unsqueeze(1).to_broadcast(spread),
-                                    in1=prod[:, 1, :].unsqueeze(1).to_broadcast(spread), op=ALU.add)
-
-        def transpose_h(n):
-            ht_ps[n] = psum_ht.tile([P, PACK, P], BF16, name="ht_ps")
-            for t in range(PACK):
-                nc.tensor.transpose(ht_ps[n][:, t, :], h_sb[n][:, t * P:(t + 1) * P], ident_bf16[:])
-
-        def group_h(n):
-            hg_sb[n] = work.tile([P, P, PACK], BF16, name="hg_sb", align_bytes=64)
-            nc.vector.tensor_copy(out=hg_sb[n][:], in_=ht_ps[n][:].rearrange("p t n -> p n t"))
-
-        def quantise_h(n):
-            codes = work.tile([P, P], U32, name="hq_codes", align_bytes=64)
-            scales = work.tile([P, P], U8, name="hq_scales", align_bytes=64)
-            nc.vector.quantize_mx(out=codes[:].bitcast(FP8X4), scales=scales[:],
-                                  in_=hg_sb[n][:].rearrange("p n t -> p (n t)"))
-            hq[n] = (codes, scales)
+            twice = [P, 2, 2, N_FREQ]
+            prod = work.tile(twice, F32, name="prod")
+            nc.vector.tensor_tensor(out=prod[:], in0=r_ps[n][:].rearrange("p (c r j) -> p c r j", c=2, r=2),
+                                    in1=cos_sin[:, n % N_POS].unsqueeze(2).to_broadcast(twice), op=ALU.mult)
+            first = k_sb[unit][:, 0, j, D_NOPE:D_NOPE + D_ROPE]
+            nc.gpsimd.tensor_tensor(out=first, in0=prod[:, 0].rearrange("p r j -> p (r j)"),
+                                    in1=prod[:, 1].rearrange("p r j -> p (r j)"), op=ALU.add)
+            nc.gpsimd.tensor_scalar(out=k_sb[unit][:, 1:HEADS, j, D_NOPE:D_NOPE + D_ROPE],
+                                    in0=first.unsqueeze(1).to_broadcast([P, HEADS - 1, D_ROPE]),
+                                    scalar1=1.0, scalar2=0.0, op0=ALU.mult, op1=ALU.add)
 
         def second_product(n):
             unit, j = divmod(n, TILES_PER_STORE)
@@ -240,7 +239,7 @@ def tile_multiheadlatentattention_pb_t_kernel(tc, x, Wkva, kv_a_norm_w, Wkvb, ou
             for kv in range(2):
                 cols = slice(kv * half_cols, (kv + 1) * half_cols)
                 kv_ps = psum_kv.tile([P, half_cols], F32, name="kv_ps")
-                nc.tensor.matmul_mx(out=kv_ps[:], lhsT=codes[:].bitcast(FP8X4), lhsT_scale=scales[:],
+                nc.tensor.matmul_mx(out=kv_ps[:], lhsT=codes.bitcast(FP8X4), lhsT_scale=scales,
                                     rhs=wb_codes[:, cols].bitcast(FP8X4), rhs_scale=wb_scales[:, cols],
                                     start=True, stop=True)
                 dst = k_sb[unit][:, :, j, 0:D_NOPE] if kv == 0 else v_sb[unit][:, :, j, :]
@@ -255,33 +254,29 @@ def tile_multiheadlatentattention_pb_t_kernel(tc, x, Wkva, kv_a_norm_w, Wkvb, ou
                 nc.sync.dma_start(out=v_groups[b, gs][:, :, i0 * v_w:(last + 1) * v_w],
                                   in_=v_sb[unit][:].rearrange("p h i d -> p h (i d)"))
 
-        def live(n):
-            return 0 <= n < N_TILES
-
         for step in range(-1, N_TILES + 3):
-            ahead, now, again, leaving = step + 1, step, step - 2, step - 3
-            if live(ahead):
-                transpose_x(ahead)
-            if live(again):
-                transpose_h(again)
-            if live(ahead):
-                group_x(ahead)
-            if live(again):
-                group_h(again)
-            if live(ahead):
-                quantise_x(ahead)
-            if live(again):
-                quantise_h(again)
-            if ahead == 0:
+            if live(step + 1):
+                transpose_x(step + 1)
+            if live(step - 2):
+                transpose_h(step - 2)
+            if live(step + 1) or live(step - 2):
+                group_both(step, step + 1, step - 2)
+            if live(step - 1):
+                normalise(step - 1)
+            if live(step + 1) or live(step - 2):
+                quantise_both(step, step + 1, step - 2)
+            if step == -1:
                 quantise_wa_rope()
-            if again in (0, 1):
-                quantise_wb(again)
-            if live(now - 1):
-                rotate(now - 1)
-            if live(now):
-                latent_product(now)
-                normalise(now)
-            if live(leaving):
-                second_product(leaving)
-            if live(now):
-                rope_product(now)
+            if step in (2, 3):
+                quantise_wb(step - 2)
+            if live(step - 1):
+                rotate(step - 1)
+            if live(step):
+                latent_product(step)
+                measure(step)
+            if step in (1, 2):
+                group_wb(step - 1)
+            if live(step - 3):
+                second_product(step - 3)
+            if live(step):
+                rope_product(step)

@@ -59,21 +59,22 @@ def tile_multiheadlatentattention_pb_t_kernel(tc, x, Wkva, kv_a_norm_w, Wkvb, ou
             out=wa_raw[:].rearrange("q (u e) c -> q u (e c)", u=2),
             in_=Wkva.rearrange("(u q e) c -> q u (e c)", u=2, e=2),
         )
+        wb_raw = consts.tile([P, PACK, HEADS * (D_NOPE + D_V)], BF16)
+        nc.sync.dma_start(out=wb_raw[:], in_=Wkvb.rearrange("(t p) n -> p t n", p=P))
         x_sb = []
         for g in range(N_GROUPS):
             x_tile = x_pool.tile([P, TILES_PER_GROUP * D_MODEL], BF16, name="x_sb%d" % g)
+            nc.sync.dma_start(out=x_tile[:], in_=x_groups[g])
             x_sb.append(x_tile)
-        nc.sync.dma_start(out=x_sb[0][:], in_=x_groups[0])
-        gain_bc = consts.tile([P, R_KV], BF16)
-        nc.scalar.dma_start(out=gain_bc[:], in_=kv_a_norm_w.partition_broadcast(P))
-        wb_raw = consts.tile([P, PACK, HEADS * (D_NOPE + D_V)], BF16)
-        nc.sync.dma_start(out=wb_raw[:], in_=Wkvb.rearrange("(t p) n -> p t n", p=P))
-        for g in range(1, N_GROUPS):
-            nc.sync.dma_start(out=x_sb[g][:], in_=x_groups[g])
 
         pos_i = consts.tile([P, N_POS], I32)
         nc.gpsimd.iota(pos_i[:], pattern=[[GROUP, GROUPS_PER_SEQ], [1, TILES_PER_GROUP]], base=0,
                        channel_multiplier=TILES_PER_GROUP)
+        gain_rows = consts.tile([P, R_KV], BF16)
+        nc.gpsimd.memset(gain_rows[:].bitcast(F32), 0.0)
+        nc.scalar.dma_start(out=gain_rows[0:1, :], in_=kv_a_norm_w.rearrange("(o k) -> o k", o=1))
+        ones = consts.tile([P, P], BF16)
+        nc.gpsimd.memset(ones[:], 1.0)
         ident_f32 = consts.tile([P, P], F32)
         make_identity(nc, ident_f32[:])
         ident_bf16 = consts.tile([P, P], BF16)
@@ -108,6 +109,9 @@ def tile_multiheadlatentattention_pb_t_kernel(tc, x, Wkva, kv_a_norm_w, Wkvb, ou
         nc.scalar.activation(out=cos_sin[:], in_=half_sq[:].rearrange("p c s j -> p s c j"), func=ACT.Copy,
                              bias=1.0, scale=-2.0)
 
+        gain_ps = psum_c.tile([P, R_KV], F32, name="c_ps")
+        nc.tensor.matmul(out=gain_ps[:], lhsT=ones[:], rhs=gain_rows[:], start=True, stop=True)
+
         wa_cols = R_KV + 2 * D_ROPE
         wa_grouped = consts.tile([P, wa_cols, PACK], BF16, align_bytes=64)
         wa_codes = consts.tile([P, wa_cols], U32, align_bytes=64)
@@ -115,6 +119,8 @@ def tile_multiheadlatentattention_pb_t_kernel(tc, x, Wkva, kv_a_norm_w, Wkvb, ou
         nc.vector.tensor_copy(out=wa_grouped[:, 0:R_KV, :], in_=wa_raw[:, :, 0:R_KV].rearrange("p t c -> p c t"))
         nc.vector.quantize_mx(out=wa_codes[:, 0:R_KV].bitcast(FP8X4), scales=wa_scales[:, 0:R_KV],
                               in_=wa_grouped[:, 0:R_KV, :].rearrange("p c t -> p (c t)"))
+        gain_bc = consts.tile([P, R_KV], BF16)
+        nc.vector.tensor_copy(out=gain_bc[:], in_=gain_ps[:])
         rope_raw = wa_raw[:, :, R_KV:R_KV + D_ROPE]
         raw_pairs = rope_raw.rearrange("p t (i two) -> p i two t", two=2)
         rot_pairs = wa_grouped[:, R_KV + D_ROPE:wa_cols, :].rearrange("p (i two) t -> p i two t", two=2)
@@ -124,10 +130,6 @@ def tile_multiheadlatentattention_pb_t_kernel(tc, x, Wkva, kv_a_norm_w, Wkvb, ou
                                 op0=ALU.mult, op1=ALU.add)
         nc.gpsimd.tensor_scalar(out=rot_pairs[:, :, 1, :], in0=raw_pairs[:, :, 0, :], scalar1=1.0, scalar2=0.0,
                                 op0=ALU.mult, op1=ALU.add)
-
-        def quantise_wa_rope():
-            nc.vector.quantize_mx(out=wa_codes[:, R_KV:wa_cols].bitcast(FP8X4), scales=wa_scales[:, R_KV:wa_cols],
-                                  in_=wa_grouped[:, R_KV:wa_cols, :].rearrange("p c t -> p (c t)"))
 
         wb_cols = HEADS * (D_NOPE + D_V)
         half_cols = wb_cols // 2
@@ -148,6 +150,9 @@ def tile_multiheadlatentattention_pb_t_kernel(tc, x, Wkva, kv_a_norm_w, Wkvb, ou
             cols = slice(kv * half_cols, (kv + 1) * half_cols)
             nc.vector.quantize_mx(out=wb_codes[:, cols].bitcast(FP8X4), scales=wb_scales[:, cols],
                                   in_=wb_grouped[:, cols, :].rearrange("p c t -> p (c t)"))
+
+        group_wb(0)
+        group_wb(1)
 
         xt_ps, c_ps, r_ps, inv_rms, h_sb, ht_ps, grouped, xq, hq, k_sb, v_sb = {}, {}, {}, {}, {}, {}, {}, {}, {}, {}, {}
 
@@ -254,7 +259,7 @@ def tile_multiheadlatentattention_pb_t_kernel(tc, x, Wkva, kv_a_norm_w, Wkvb, ou
                 nc.sync.dma_start(out=v_groups[b, gs][:, :, i0 * v_w:(last + 1) * v_w],
                                   in_=v_sb[unit][:].rearrange("p h i d -> p h (i d)"))
 
-        for step in range(-1, N_TILES + 3):
+        def one_step(step):
             if live(step + 1):
                 transpose_x(step + 1)
             if live(step - 2):
@@ -265,18 +270,21 @@ def tile_multiheadlatentattention_pb_t_kernel(tc, x, Wkva, kv_a_norm_w, Wkvb, ou
                 normalise(step - 1)
             if live(step + 1) or live(step - 2):
                 quantise_both(step, step + 1, step - 2)
-            if step == -1:
-                quantise_wa_rope()
-            if step in (2, 3):
-                quantise_wb(step - 2)
             if live(step - 1):
                 rotate(step - 1)
             if live(step):
                 latent_product(step)
                 measure(step)
-            if step in (1, 2):
-                group_wb(step - 1)
             if live(step - 3):
                 second_product(step - 3)
             if live(step):
                 rope_product(step)
+
+        one_step(-1)
+        nc.vector.quantize_mx(out=wa_codes[:, R_KV:wa_cols].bitcast(FP8X4), scales=wa_scales[:, R_KV:wa_cols],
+                              in_=wa_grouped[:, R_KV:wa_cols, :].rearrange("p c t -> p (c t)"))
+        quantise_wb(0)
+        one_step(0)
+        quantise_wb(1)
+        for step in range(1, N_TILES + 3):
+            one_step(step)

@@ -54,6 +54,13 @@ def tile_multiheadlatentattention_pb_t_kernel(tc, x, Wkva, kv_a_norm_w, Wkvb, ou
         psum_ht = ctx.enter_context(tc.psum_pool(name="psum_ht", bufs=1))
         psum_kv = ctx.enter_context(tc.psum_pool(name="psum_kv", bufs=2))
 
+        pos_i = consts.tile([P, N_POS], I32)
+        nc.gpsimd.iota(pos_i[:], pattern=[[GROUP, GROUPS_PER_SEQ], [1, TILES_PER_GROUP]], base=0,
+                       channel_multiplier=TILES_PER_GROUP)
+
+        gain_rows = consts.tile([P, R_KV], BF16)
+        nc.gpsimd.memset(gain_rows[:].bitcast(F32), 0.0)
+        nc.sync.dma_start(out=gain_rows[0:1, :], in_=kv_a_norm_w.rearrange("(o k) -> o k", o=1))
         wa_raw = consts.tile([P, PACK, R_KV + D_ROPE], BF16)
         nc.sync.dma_start(
             out=wa_raw[:].rearrange("q (u e) c -> q u (e c)", u=2),
@@ -67,12 +74,6 @@ def tile_multiheadlatentattention_pb_t_kernel(tc, x, Wkva, kv_a_norm_w, Wkvb, ou
             nc.sync.dma_start(out=x_tile[:], in_=x_groups[g])
             x_sb.append(x_tile)
 
-        pos_i = consts.tile([P, N_POS], I32)
-        nc.gpsimd.iota(pos_i[:], pattern=[[GROUP, GROUPS_PER_SEQ], [1, TILES_PER_GROUP]], base=0,
-                       channel_multiplier=TILES_PER_GROUP)
-        gain_rows = consts.tile([P, R_KV], BF16)
-        nc.gpsimd.memset(gain_rows[:].bitcast(F32), 0.0)
-        nc.scalar.dma_start(out=gain_rows[0:1, :], in_=kv_a_norm_w.rearrange("(o k) -> o k", o=1))
         ones = consts.tile([P, P], BF16)
         nc.gpsimd.memset(ones[:], 1.0)
         ident_f32 = consts.tile([P, P], F32)
@@ -154,7 +155,8 @@ def tile_multiheadlatentattention_pb_t_kernel(tc, x, Wkva, kv_a_norm_w, Wkvb, ou
         group_wb(0)
         group_wb(1)
 
-        xt_ps, c_ps, r_ps, inv_rms, h_sb, ht_ps, grouped, xq, hq, k_sb, v_sb = {}, {}, {}, {}, {}, {}, {}, {}, {}, {}, {}
+        xt_ps, c_ps, r_ps, inv_rms, h_sb, ht_ps, grouped, xq, hq, prod = {}, {}, {}, {}, {}, {}, {}, {}, {}, {}
+        k_sb, v_sb = {}, {}
 
         def live(n):
             return 0 <= n < N_TILES
@@ -223,17 +225,19 @@ def tile_multiheadlatentattention_pb_t_kernel(tc, x, Wkva, kv_a_norm_w, Wkvb, ou
                                            op0=ALU.mult, op1=ALU.mult)
 
         def rotate(n):
+            twice = [P, 2, 2, N_FREQ]
+            prod[n] = work.tile(twice, F32, name="prod")
+            nc.vector.tensor_tensor(out=prod[n][:], in0=r_ps[n][:].rearrange("p (c r j) -> p c r j", c=2, r=2),
+                                    in1=cos_sin[:, n % N_POS].unsqueeze(2).to_broadcast(twice), op=ALU.mult)
+
+        def spread(n):
             unit, j = divmod(n, TILES_PER_STORE)
             if j == 0:
                 k_sb[unit] = outs.tile([P, HEADS, TILES_PER_STORE, D_NOPE + D_ROPE], F32, name="k_sb")
                 v_sb[unit] = outs.tile([P, HEADS, TILES_PER_STORE, D_V], F32, name="v_sb")
-            twice = [P, 2, 2, N_FREQ]
-            prod = work.tile(twice, F32, name="prod")
-            nc.vector.tensor_tensor(out=prod[:], in0=r_ps[n][:].rearrange("p (c r j) -> p c r j", c=2, r=2),
-                                    in1=cos_sin[:, n % N_POS].unsqueeze(2).to_broadcast(twice), op=ALU.mult)
             first = k_sb[unit][:, 0, j, D_NOPE:D_NOPE + D_ROPE]
-            nc.gpsimd.tensor_tensor(out=first, in0=prod[:, 0].rearrange("p r j -> p (r j)"),
-                                    in1=prod[:, 1].rearrange("p r j -> p (r j)"), op=ALU.add)
+            nc.vector.tensor_tensor(out=first, in0=prod[n][:, 0].rearrange("p r j -> p (r j)"),
+                                    in1=prod[n][:, 1].rearrange("p r j -> p (r j)"), op=ALU.add)
             nc.gpsimd.tensor_scalar(out=k_sb[unit][:, 1:HEADS, j, D_NOPE:D_NOPE + D_ROPE],
                                     in0=first.unsqueeze(1).to_broadcast([P, HEADS - 1, D_ROPE]),
                                     scalar1=1.0, scalar2=0.0, op0=ALU.mult, op1=ALU.add)
@@ -262,21 +266,23 @@ def tile_multiheadlatentattention_pb_t_kernel(tc, x, Wkva, kv_a_norm_w, Wkvb, ou
         def one_step(step):
             if live(step + 1):
                 transpose_x(step + 1)
-            if live(step - 2):
-                transpose_h(step - 2)
-            if live(step + 1) or live(step - 2):
-                group_both(step, step + 1, step - 2)
+            if live(step - 3):
+                transpose_h(step - 3)
+            if live(step + 1) or live(step - 3):
+                group_both(step, step + 1, step - 3)
             if live(step - 1):
                 normalise(step - 1)
-            if live(step + 1) or live(step - 2):
-                quantise_both(step, step + 1, step - 2)
+            if live(step + 1) or live(step - 3):
+                quantise_both(step, step + 1, step - 3)
             if live(step - 1):
                 rotate(step - 1)
+            if live(step - 2):
+                spread(step - 2)
             if live(step):
                 latent_product(step)
                 measure(step)
-            if live(step - 3):
-                second_product(step - 3)
+            if live(step - 4):
+                second_product(step - 4)
             if live(step):
                 rope_product(step)
 
@@ -286,5 +292,5 @@ def tile_multiheadlatentattention_pb_t_kernel(tc, x, Wkva, kv_a_norm_w, Wkvb, ou
         quantise_wb(0)
         one_step(0)
         quantise_wb(1)
-        for step in range(1, N_TILES + 3):
+        for step in range(1, N_TILES + 4):
             one_step(step)

@@ -67,7 +67,10 @@ def tile_multiheadlatentattention_pb_t_kernel(tc, x, Wkva, kv_a_norm_w, Wkvb, ou
             in_=Wkva.rearrange("(u q e) c -> q u (e c)", u=2, e=2),
         )
         wb_raw = consts.tile([P, PACK, HEADS * (D_NOPE + D_V)], BF16)
-        nc.sync.dma_start(out=wb_raw[:], in_=Wkvb.rearrange("(t p) n -> p t n", p=P))
+        nc.sync.dma_start(
+            out=wb_raw[:].rearrange("q (u e) c -> q u (e c)", u=2),
+            in_=Wkvb.rearrange("(u q e) c -> q u (e c)", u=2, e=2),
+        )
         x_sb = []
         for g in range(N_GROUPS):
             x_tile = x_pool.tile([P, TILES_PER_GROUP * D_MODEL], BF16, name="x_sb%d" % g)
@@ -78,8 +81,6 @@ def tile_multiheadlatentattention_pb_t_kernel(tc, x, Wkva, kv_a_norm_w, Wkvb, ou
         nc.gpsimd.memset(ones[:], 1.0)
         ident_f32 = consts.tile([P, P], F32)
         make_identity(nc, ident_f32[:])
-        ident_bf16 = consts.tile([P, P], BF16)
-        make_identity(nc, ident_bf16[:])
         eps_col = consts.tile([P, 1], F32)
         nc.vector.memset(eps_col[:], EPS)
 
@@ -170,9 +171,10 @@ def tile_multiheadlatentattention_pb_t_kernel(tc, x, Wkva, kv_a_norm_w, Wkvb, ou
                 nc.tensor.transpose(xt_ps[n][:, u, :], words[:, first:first + P], ident_f32[:])
 
         def transpose_h(n):
-            ht_ps[n] = psum_ht.tile([P, PACK, P], BF16, name="ht_ps")
-            for t in range(PACK):
-                nc.tensor.transpose(ht_ps[n][:, t, :], h_sb[n][:, t * P:(t + 1) * P], ident_bf16[:])
+            words = h_sb[n][:].bitcast(F32)
+            ht_ps[n] = psum_ht.tile([P, 2, P], F32, name="ht_ps")
+            for u in range(2):
+                nc.tensor.transpose(ht_ps[n][:, u, :], words[:, u * P:(u + 1) * P], ident_f32[:])
 
         def group_both(step, nx, nh):
             grouped[step] = work.tile([P, 2 * P * PACK], BF16, name="grouped", align_bytes=64)
@@ -184,8 +186,8 @@ def tile_multiheadlatentattention_pb_t_kernel(tc, x, Wkva, kv_a_norm_w, Wkvb, ou
                 else:
                     nc.scalar.copy(out=dst, in_=src)
             if live(nh):
-                nc.vector.tensor_copy(out=grouped[step][:, P * PACK:].rearrange("p (n t) -> p n t", t=PACK),
-                                      in_=ht_ps[nh][:].rearrange("p t n -> p n t"))
+                nc.vector.tensor_copy(out=grouped[step][:].bitcast(F32)[:, 2 * P:4 * P].rearrange("p (n u) -> p n u", u=2),
+                                      in_=ht_ps[nh][:].rearrange("p u n -> p n u"))
 
         def quantise_both(step, nx, nh):
             codes = work.tile([P, 2 * P], U32, name="codes", align_bytes=64)

@@ -48,39 +48,39 @@ def tile_multiheadlatentattention_pb_t_kernel(tc, x, Wkva, kv_a_norm_w, Wkvb, ou
         work = ctx.enter_context(tc.tile_pool(name="work", bufs=4))
         small = ctx.enter_context(tc.tile_pool(name="small", bufs=8))
         outs = ctx.enter_context(tc.tile_pool(name="outs", bufs=6))
-        psum_xt = ctx.enter_context(tc.psum_pool(name="psum_xt", bufs=1))
+        psum_xh = ctx.enter_context(tc.psum_pool(name="psum_xh", bufs=1))
         psum_c = ctx.enter_context(tc.psum_pool(name="psum_c", bufs=2))
         psum_r = ctx.enter_context(tc.psum_pool(name="psum_r", bufs=2))
-        psum_ht = ctx.enter_context(tc.psum_pool(name="psum_ht", bufs=1))
-        psum_kv = ctx.enter_context(tc.psum_pool(name="psum_kv", bufs=2))
+        psum_kv = ctx.enter_context(tc.psum_pool(name="psum_kv", bufs=3))
 
         pos_i = consts.tile([P, N_POS], I32)
         nc.gpsimd.iota(pos_i[:], pattern=[[GROUP, GROUPS_PER_SEQ], [1, TILES_PER_GROUP]], base=0,
                        channel_multiplier=TILES_PER_GROUP)
-
+        ident_f32 = consts.tile([P, P], F32)
+        make_identity(nc, ident_f32[:])
         gain_rows = consts.tile([P, R_KV], BF16)
         nc.gpsimd.memset(gain_rows[:].bitcast(F32), 0.0)
-        nc.sync.dma_start(out=gain_rows[0:1, :], in_=kv_a_norm_w.rearrange("(o k) -> o k", o=1))
+
         wa_raw = consts.tile([P, PACK, R_KV + D_ROPE], BF16)
         nc.sync.dma_start(
             out=wa_raw[:].rearrange("q (u e) c -> q u (e c)", u=2),
             in_=Wkva.rearrange("(u q e) c -> q u (e c)", u=2, e=2),
         )
         wb_raw = consts.tile([P, PACK, HEADS * (D_NOPE + D_V)], BF16)
-        nc.sync.dma_start(
-            out=wb_raw[:].rearrange("q (u e) c -> q u (e c)", u=2),
-            in_=Wkvb.rearrange("(u q e) c -> q u (e c)", u=2, e=2),
-        )
         x_sb = []
         for g in range(N_GROUPS):
             x_tile = x_pool.tile([P, TILES_PER_GROUP * D_MODEL], BF16, name="x_sb%d" % g)
             nc.sync.dma_start(out=x_tile[:], in_=x_groups[g])
             x_sb.append(x_tile)
+            if g == 0:
+                nc.sync.dma_start(out=gain_rows[0:1, :], in_=kv_a_norm_w.rearrange("(o k) -> o k", o=1))
+                nc.sync.dma_start(
+                    out=wb_raw[:].rearrange("q (u e) c -> q u (e c)", u=2),
+                    in_=Wkvb.rearrange("(u q e) c -> q u (e c)", u=2, e=2),
+                )
 
         ones = consts.tile([P, P], BF16)
         nc.gpsimd.memset(ones[:], 1.0)
-        ident_f32 = consts.tile([P, P], F32)
-        make_identity(nc, ident_f32[:])
         eps_col = consts.tile([P, 1], F32)
         nc.vector.memset(eps_col[:], EPS)
 
@@ -101,18 +101,16 @@ def tile_multiheadlatentattention_pb_t_kernel(tc, x, Wkva, kv_a_norm_w, Wkvb, ou
         nc.vector.tensor_scalar(out=whole[:], in0=turns[:], scalar1=ROUND_MAGIC, scalar2=ROUND_MAGIC,
                                 op0=ALU.add, op1=ALU.subtract)
         part = trig.tile([P, 2, N_POS, N_FREQ], F32)
-        nc.vector.tensor_tensor(out=part[:, 0], in0=turns[:], in1=whole[:], op=ALU.subtract)
-        nc.vector.tensor_scalar(out=part[:, 1], in0=part[:, 0], scalar1=0.25, scalar2=None, op0=ALU.subtract)
-        half_sin = trig.tile([P, 2, N_POS, N_FREQ], F32)
-        nc.scalar.activation(out=half_sin[:], in_=part[:], func=ACT.Sin, scale=math.pi)
-        half_sq = trig.tile([P, 2, N_POS, N_FREQ], F32)
-        nc.scalar.activation(out=half_sq[:], in_=half_sin[:], func=ACT.Square)
+        nc.vector.tensor_tensor(out=part[:, 1], in0=turns[:], in1=whole[:], op=ALU.subtract)
+        over = trig.tile(shape, F32)
+        nc.vector.tensor_scalar(out=over[:], in0=part[:, 1], scalar1=0.25, scalar2=None, op0=ALU.is_gt)
+        nc.vector.scalar_tensor_tensor(out=part[:, 0], in0=part[:, 1], scalar=0.25, in1=over[:],
+                                       op0=ALU.add, op1=ALU.subtract)
         cos_sin = consts.tile([P, N_POS, 2, N_FREQ], F32)
-        nc.scalar.activation(out=cos_sin[:], in_=half_sq[:].rearrange("p c s j -> p s c j"), func=ACT.Copy,
-                             bias=1.0, scale=-2.0)
-
-        gain_ps = psum_c.tile([P, R_KV], F32, name="c_ps")
-        nc.tensor.matmul(out=gain_ps[:], lhsT=ones[:], rhs=gain_rows[:], start=True, stop=True)
+        for c in (1, 0):
+            nc.scalar.activation(out=cos_sin[:, :, c, :], in_=part[:, c], func=ACT.Sin, scale=2.0 * math.pi)
+        table_warmer = trig.tile([P, 1], F32)
+        nc.scalar.activation(out=table_warmer[:], in_=eps_col[:], func=ACT.Abs_reciprocal_sqrt)
 
         wa_cols = R_KV + 2 * D_ROPE
         wa_grouped = consts.tile([P, wa_cols, PACK], BF16, align_bytes=64)
@@ -121,8 +119,6 @@ def tile_multiheadlatentattention_pb_t_kernel(tc, x, Wkva, kv_a_norm_w, Wkvb, ou
         nc.vector.tensor_copy(out=wa_grouped[:, 0:R_KV, :], in_=wa_raw[:, :, 0:R_KV].rearrange("p t c -> p c t"))
         nc.vector.quantize_mx(out=wa_codes[:, 0:R_KV].bitcast(FP8X4), scales=wa_scales[:, 0:R_KV],
                               in_=wa_grouped[:, 0:R_KV, :].rearrange("p c t -> p (c t)"))
-        gain_bc = consts.tile([P, R_KV], BF16)
-        nc.vector.tensor_copy(out=gain_bc[:], in_=gain_ps[:])
         rope_raw = wa_raw[:, :, R_KV:R_KV + D_ROPE]
         raw_pairs = rope_raw.rearrange("p t (i two) -> p i two t", two=2)
         rot_pairs = wa_grouped[:, R_KV + D_ROPE:wa_cols, :].rearrange("p (i two) t -> p i two t", two=2)
@@ -140,54 +136,49 @@ def tile_multiheadlatentattention_pb_t_kernel(tc, x, Wkva, kv_a_norm_w, Wkvb, ou
         wb_scales = consts.tile([P, wb_cols], U8, align_bytes=64)
         wb_parts = wb_raw[:].rearrange("p t (h kv d) -> p kv h d t", kv=2, d=D_NOPE)
 
-        def group_wb(kv):
+        def group_wb(kv, heads):
             cols = slice(kv * half_cols, (kv + 1) * half_cols)
             dst = wb_grouped[:, cols, :].rearrange("p (h d) t -> p h d t", h=HEADS)
             if kv == 0:
-                nc.vector.tensor_copy(out=dst, in_=wb_parts[:, kv])
+                nc.gpsimd.tensor_scalar(out=dst[:, heads], in0=wb_parts[:, kv, heads], scalar1=1.0, scalar2=0.0,
+                                        op0=ALU.mult, op1=ALU.add)
             else:
-                nc.scalar.copy(out=dst, in_=wb_parts[:, kv])
+                nc.scalar.copy(out=dst[:, heads], in_=wb_parts[:, kv, heads])
 
         def quantise_wb(kv):
             cols = slice(kv * half_cols, (kv + 1) * half_cols)
             nc.vector.quantize_mx(out=wb_codes[:, cols].bitcast(FP8X4), scales=wb_scales[:, cols],
                                   in_=wb_grouped[:, cols, :].rearrange("p c t -> p (c t)"))
 
-        group_wb(0)
-        group_wb(1)
+        group_wb(0, slice(0, 2))
+        group_wb(0, slice(2, 4))
 
-        xt_ps, c_ps, r_ps, inv_rms, h_sb, ht_ps, grouped, xq, hq, prod = {}, {}, {}, {}, {}, {}, {}, {}, {}, {}
+        xh_ps, c_ps, r_ps, inv_rms, h_sb, grouped, xq, hq, prod = {}, {}, {}, {}, {}, {}, {}, {}, {}
         k_sb, v_sb = {}, {}
 
         def live(n):
             return 0 <= n < N_TILES
 
-        def transpose_x(n):
-            g, i = divmod(n, TILES_PER_GROUP)
-            words = x_sb[g][:].bitcast(F32)
-            xt_ps[n] = psum_xt.tile([P, 2, P], F32, name="xt_ps")
-            for u in range(2):
-                first = (i * 2 + u) * P
-                nc.tensor.transpose(xt_ps[n][:, u, :], words[:, first:first + P], ident_f32[:])
-
-        def transpose_h(n):
-            words = h_sb[n][:].bitcast(F32)
-            ht_ps[n] = psum_ht.tile([P, 2, P], F32, name="ht_ps")
-            for u in range(2):
-                nc.tensor.transpose(ht_ps[n][:, u, :], words[:, u * P:(u + 1) * P], ident_f32[:])
+        def transpose_both(step, nx, nh):
+            xh_ps[step] = psum_xh.tile([P, 4, P], F32, name="xh_ps")
+            if live(nx):
+                g, i = divmod(nx, TILES_PER_GROUP)
+                words = x_sb[g][:].bitcast(F32)
+                for u in range(2):
+                    first = (i * 2 + u) * P
+                    nc.tensor.transpose(xh_ps[step][:, u, :], words[:, first:first + P], ident_f32[:])
+            if live(nh):
+                words = h_sb[nh][:].bitcast(F32)
+                for u in range(2):
+                    nc.tensor.transpose(xh_ps[step][:, 2 + u, :], words[:, u * P:(u + 1) * P], ident_f32[:])
 
         def group_both(step, nx, nh):
             grouped[step] = work.tile([P, 2 * P * PACK], BF16, name="grouped", align_bytes=64)
-            if live(nx):
-                dst = grouped[step][:].bitcast(F32)[:, 0:2 * P].rearrange("p (n u) -> p n u", u=2)
-                src = xt_ps[nx][:].rearrange("p u n -> p n u")
-                if nx % 2 == 0:
-                    nc.vector.tensor_copy(out=dst, in_=src)
-                else:
-                    nc.scalar.copy(out=dst, in_=src)
-            if live(nh):
-                nc.vector.tensor_copy(out=grouped[step][:].bitcast(F32)[:, 2 * P:4 * P].rearrange("p (n u) -> p n u", u=2),
-                                      in_=ht_ps[nh][:].rearrange("p u n -> p n u"))
+            lo = 0 if live(nx) else 2
+            hi = 4 if live(nh) else 2
+            nc.vector.tensor_copy(
+                out=grouped[step][:].bitcast(F32)[:, lo * P:hi * P].rearrange("p (w n u) -> p w n u", n=P, u=2),
+                in_=xh_ps[step][:, lo:hi, :].rearrange("p (w u) n -> p w n u", u=2))
 
         def quantise_both(step, nx, nh):
             codes = work.tile([P, 2 * P], U32, name="codes", align_bytes=64)
@@ -238,7 +229,7 @@ def tile_multiheadlatentattention_pb_t_kernel(tc, x, Wkva, kv_a_norm_w, Wkvb, ou
                 k_sb[unit] = outs.tile([P, HEADS, TILES_PER_STORE, D_NOPE + D_ROPE], F32, name="k_sb")
                 v_sb[unit] = outs.tile([P, HEADS, TILES_PER_STORE, D_V], F32, name="v_sb")
             first = k_sb[unit][:, 0, j, D_NOPE:D_NOPE + D_ROPE]
-            nc.vector.tensor_tensor(out=first, in0=prod[n][:, 0].rearrange("p r j -> p (r j)"),
+            nc.gpsimd.tensor_tensor(out=first, in0=prod[n][:, 0].rearrange("p r j -> p (r j)"),
                                     in1=prod[n][:, 1].rearrange("p r j -> p (r j)"), op=ALU.add)
             nc.gpsimd.tensor_scalar(out=k_sb[unit][:, 1:HEADS, j, D_NOPE:D_NOPE + D_ROPE],
                                     in0=first.unsqueeze(1).to_broadcast([P, HEADS - 1, D_ROPE]),
@@ -266,11 +257,8 @@ def tile_multiheadlatentattention_pb_t_kernel(tc, x, Wkva, kv_a_norm_w, Wkvb, ou
                                   in_=v_sb[unit][:].rearrange("p h i d -> p h (i d)"))
 
         def one_step(step):
-            if live(step + 1):
-                transpose_x(step + 1)
-            if live(step - 3):
-                transpose_h(step - 3)
             if live(step + 1) or live(step - 3):
+                transpose_both(step, step + 1, step - 3)
                 group_both(step, step + 1, step - 3)
             if live(step - 1):
                 normalise(step - 1)
@@ -289,10 +277,19 @@ def tile_multiheadlatentattention_pb_t_kernel(tc, x, Wkva, kv_a_norm_w, Wkvb, ou
                 rope_product(step)
 
         one_step(-1)
+        gain_ps = psum_c.tile([P, R_KV], F32, name="c_ps")
+        nc.tensor.matmul(out=gain_ps[:], lhsT=ones[:], rhs=gain_rows[:], start=True, stop=True)
+        gain_bc = consts.tile([P, R_KV], BF16)
         nc.vector.quantize_mx(out=wa_codes[:, R_KV:wa_cols].bitcast(FP8X4), scales=wa_scales[:, R_KV:wa_cols],
                               in_=wa_grouped[:, R_KV:wa_cols, :].rearrange("p c t -> p (c t)"))
-        quantise_wb(0)
+        nc.vector.tensor_copy(out=gain_bc[:], in_=gain_ps[:])
         one_step(0)
+        group_wb(1, slice(0, 2))
+        one_step(1)
+        group_wb(1, slice(2, 4))
+        one_step(2)
+        quantise_wb(0)
+        one_step(3)
         quantise_wb(1)
-        for step in range(1, N_TILES + 4):
+        for step in range(4, N_TILES + 4):
             one_step(step)

@@ -229,7 +229,7 @@ def tile_multiheadlatentattention_pb_t_kernel(tc, x, Wkva, kv_a_norm_w, Wkvb, ou
                 k_sb[unit] = outs.tile([P, HEADS, TILES_PER_STORE, D_NOPE + D_ROPE], F32, name="k_sb")
                 v_sb[unit] = outs.tile([P, HEADS, TILES_PER_STORE, D_V], F32, name="v_sb")
             first = k_sb[unit][:, 0, j, D_NOPE:D_NOPE + D_ROPE]
-            nc.gpsimd.tensor_tensor(out=first, in0=prod[n][:, 0].rearrange("p r j -> p (r j)"),
+            nc.vector.tensor_tensor(out=first, in0=prod[n][:, 0].rearrange("p r j -> p (r j)"),
                                     in1=prod[n][:, 1].rearrange("p r j -> p (r j)"), op=ALU.add)
             nc.gpsimd.tensor_scalar(out=k_sb[unit][:, 1:HEADS, j, D_NOPE:D_NOPE + D_ROPE],
                                     in0=first.unsqueeze(1).to_broadcast([P, HEADS - 1, D_ROPE]),

@@ -82,21 +82,16 @@ def tile_multiheadlatentattention_pb_t_kernel(tc, x, Wkva, kv_a_norm_w, Wkvb, ou
         ones = consts.tile([P, P], BF16)
         nc.gpsimd.memset(ones[:], 1.0)
         eps_col = consts.tile([P, 1], F32)
-        nc.vector.memset(eps_col[:], EPS)
+        nc.gpsimd.memset(eps_col[:], EPS)
 
         shape = [P, N_POS, N_FREQ]
-        pos = trig.tile([P, N_POS], F32)
-        nc.vector.tensor_copy(out=pos[:], in_=pos_i[:])
-        freq = trig.tile([P, N_FREQ], F32)
-        nc.vector.memset(freq[:, 0:1], 1.0)
+        turns = trig.tile(shape, F32)
+        nc.vector.tensor_scalar(out=turns[:, :, 0:1], in0=pos_i[:].unsqueeze(2), scalar1=0.5 / math.pi, scalar2=None,
+                                op0=ALU.mult)
         for doubling in range(6):
             have = 2**doubling
-            nc.vector.tensor_scalar(out=freq[:, have:2 * have], in0=freq[:, 0:have],
+            nc.vector.tensor_scalar(out=turns[:, :, have:2 * have], in0=turns[:, :, 0:have],
                                     scalar1=ROPE_BASE ** (-have / N_FREQ), scalar2=None, op0=ALU.mult)
-        turns = trig.tile(shape, F32)
-        nc.vector.scalar_tensor_tensor(out=turns[:], in0=freq[:].unsqueeze(1).to_broadcast(shape),
-                                       scalar=0.5 / math.pi, in1=pos[:].unsqueeze(2).to_broadcast(shape),
-                                       op0=ALU.mult, op1=ALU.mult)
         whole = trig.tile(shape, F32)
         nc.vector.tensor_scalar(out=whole[:], in0=turns[:], scalar1=ROUND_MAGIC, scalar2=ROUND_MAGIC,
                                 op0=ALU.add, op1=ALU.subtract)
@@ -153,7 +148,7 @@ def tile_multiheadlatentattention_pb_t_kernel(tc, x, Wkva, kv_a_norm_w, Wkvb, ou
         group_wb(0, slice(0, 2))
         group_wb(0, slice(2, 4))
 
-        xh_ps, c_ps, r_ps, inv_rms, h_sb, grouped, xq, hq, prod = {}, {}, {}, {}, {}, {}, {}, {}, {}
+        xh_ps, c_ps, r_ps, sum_sq, inv_rms, h_sb, grouped, xq, hq, prod = {}, {}, {}, {}, {}, {}, {}, {}, {}, {}
         k_sb, v_sb = {}, {}
 
         def live(n):
@@ -204,12 +199,14 @@ def tile_multiheadlatentattention_pb_t_kernel(tc, x, Wkva, kv_a_norm_w, Wkvb, ou
                                 rhs=wa_codes[:, R_KV:wa_cols].bitcast(FP8X4), rhs_scale=wa_scales[:, R_KV:wa_cols],
                                 start=True, stop=True)
 
-        def measure(n):
+        def sum_squares(n):
             squares = work.tile([P, R_KV], BF16, name="squares")
-            sum_sq = small.tile([P, 1], F32, name="sum_sq")
-            nc.scalar.activation(out=squares[:], in_=c_ps[n][:], func=ACT.Square, accum_out=sum_sq[:])
+            sum_sq[n] = small.tile([P, 1], F32, name="sum_sq")
+            nc.scalar.activation(out=squares[:], in_=c_ps[n][:], func=ACT.Square, accum_out=sum_sq[n][:])
+
+        def invert_rms(n):
             inv_rms[n] = small.tile([P, 1], F32, name="inv_rms")
-            nc.scalar.activation(out=inv_rms[n][:], in_=sum_sq[:], func=ACT.Abs_reciprocal_sqrt, bias=eps_col[:],
+            nc.scalar.activation(out=inv_rms[n][:], in_=sum_sq[n][:], func=ACT.Abs_reciprocal_sqrt, bias=eps_col[:],
                                  scale=1.0 / R_KV)
 
         def normalise(n):
@@ -235,10 +232,10 @@ def tile_multiheadlatentattention_pb_t_kernel(tc, x, Wkva, kv_a_norm_w, Wkvb, ou
                                     in0=first.unsqueeze(1).to_broadcast([P, HEADS - 1, D_ROPE]),
                                     scalar1=1.0, scalar2=0.0, op0=ALU.mult, op1=ALU.add)
 
-        def second_product(n):
+        def second_product(n, kv_range):
             unit, j = divmod(n, TILES_PER_STORE)
             codes, scales = hq[n]
-            for kv in range(2):
+            for kv in kv_range:
                 cols = slice(kv * half_cols, (kv + 1) * half_cols)
                 kv_ps = psum_kv.tile([P, half_cols], F32, name="kv_ps")
                 nc.tensor.matmul_mx(out=kv_ps[:], lhsT=codes.bitcast(FP8X4), lhsT_scale=scales,
@@ -246,7 +243,7 @@ def tile_multiheadlatentattention_pb_t_kernel(tc, x, Wkva, kv_a_norm_w, Wkvb, ou
                                     start=True, stop=True)
                 dst = k_sb[unit][:, :, j, 0:D_NOPE] if kv == 0 else v_sb[unit][:, :, j, :]
                 nc.scalar.copy(out=dst, in_=kv_ps[:].rearrange("p (h d) -> p h d", h=HEADS))
-            if j == TILES_PER_STORE - 1:
+            if j == TILES_PER_STORE - 1 and 1 in kv_range:
                 g, last = divmod(n, TILES_PER_GROUP)
                 b, gs = divmod(g, GROUPS_PER_SEQ)
                 i0 = last + 1 - TILES_PER_STORE
@@ -264,15 +261,19 @@ def tile_multiheadlatentattention_pb_t_kernel(tc, x, Wkva, kv_a_norm_w, Wkvb, ou
                 normalise(step - 1)
             if live(step + 1) or live(step - 3):
                 quantise_both(step, step + 1, step - 3)
-            if live(step - 1):
-                rotate(step - 1)
             if live(step - 2):
                 spread(step - 2)
+            if live(step - 1):
+                rotate(step - 1)
             if live(step):
                 latent_product(step)
-                measure(step)
+                sum_squares(step)
             if live(step - 4):
-                second_product(step - 4)
+                second_product(step - 4, (0,))
+            if live(step):
+                invert_rms(step)
+            if live(step - 4):
+                second_product(step - 4, (1,))
             if live(step):
                 rope_product(step)
 

@@ -95,15 +95,12 @@ def tile_multiheadlatentattention_pb_t_kernel(tc, x, Wkva, kv_a_norm_w, Wkvb, ou
         whole = trig.tile(shape, F32)
         nc.vector.tensor_scalar(out=whole[:], in0=turns[:], scalar1=ROUND_MAGIC, scalar2=ROUND_MAGIC,
                                 op0=ALU.add, op1=ALU.subtract)
-        part = trig.tile([P, 2, N_POS, N_FREQ], F32)
-        nc.vector.tensor_tensor(out=part[:, 1], in0=turns[:], in1=whole[:], op=ALU.subtract)
-        over = trig.tile(shape, F32)
-        nc.vector.tensor_scalar(out=over[:], in0=part[:, 1], scalar1=0.25, scalar2=None, op0=ALU.is_gt)
-        nc.vector.scalar_tensor_tensor(out=part[:, 0], in0=part[:, 1], scalar=0.25, in1=over[:],
-                                       op0=ALU.add, op1=ALU.subtract)
+        part = trig.tile(shape, F32)
+        nc.vector.tensor_tensor(out=part[:], in0=turns[:], in1=whole[:], op=ALU.subtract)
         cos_sin = consts.tile([P, N_POS, 2, N_FREQ], F32)
-        for c in (1, 0):
-            nc.scalar.activation(out=cos_sin[:, :, c, :], in_=part[:, c], func=ACT.Sin, scale=2.0 * math.pi)
+        nc.scalar.activation(out=cos_sin[:, :, 1, :], in_=part[:], func=ACT.Sin, scale=2.0 * math.pi)
+        half_sin = trig.tile(shape, F32)
+        nc.scalar.activation(out=half_sin[:], in_=part[:], func=ACT.Sin, scale=math.pi)
         table_warmer = trig.tile([P, 1], F32)
         nc.scalar.activation(out=table_warmer[:], in_=eps_col[:], func=ACT.Abs_reciprocal_sqrt)
 
@@ -285,10 +282,13 @@ def tile_multiheadlatentattention_pb_t_kernel(tc, x, Wkva, kv_a_norm_w, Wkvb, ou
                               in_=wa_grouped[:, R_KV:wa_cols, :].rearrange("p c t -> p (c t)"))
         nc.vector.tensor_copy(out=gain_bc[:], in_=gain_ps[:])
         one_step(0)
-        group_wb(1, slice(0, 2))
+        half_sq = trig.tile(shape, F32)
+        nc.scalar.activation(out=half_sq[:], in_=half_sin[:], func=ACT.Square)
+        nc.scalar.activation(out=cos_sin[:, :, 0, :], in_=half_sq[:], func=ACT.Copy, bias=1.0, scale=-2.0)
         one_step(1)
-        group_wb(1, slice(2, 4))
+        group_wb(1, slice(0, 2))
         one_step(2)
+        group_wb(1, slice(2, 4))
         quantise_wb(0)
         one_step(3)
         quantise_wb(1)

@@ -88,10 +88,11 @@ def tile_multiheadlatentattention_pb_t_kernel(tc, x, Wkva, kv_a_norm_w, Wkvb, ou
         turns = trig.tile(shape, F32)
         nc.vector.tensor_scalar(out=turns[:, :, 0:1], in0=pos_i[:].unsqueeze(2), scalar1=0.5 / math.pi, scalar2=None,
                                 op0=ALU.mult)
-        for doubling in range(6):
-            have = 2**doubling
-            nc.vector.tensor_scalar(out=turns[:, :, have:2 * have], in0=turns[:, :, 0:have],
-                                    scalar1=ROPE_BASE ** (-have / N_FREQ), scalar2=None, op0=ALU.mult)
+        for level in range(3):
+            have = 4**level
+            for m in (1, 2, 3):
+                nc.vector.tensor_scalar(out=turns[:, :, m * have:(m + 1) * have], in0=turns[:, :, 0:have],
+                                        scalar1=ROPE_BASE ** (-m * have / N_FREQ), scalar2=None, op0=ALU.mult)
         whole = trig.tile(shape, F32)
         nc.vector.tensor_scalar(out=whole[:], in0=turns[:], scalar1=ROUND_MAGIC, scalar2=ROUND_MAGIC,
                                 op0=ALU.add, op1=ALU.subtract)
@@ -109,8 +110,6 @@ def tile_multiheadlatentattention_pb_t_kernel(tc, x, Wkva, kv_a_norm_w, Wkvb, ou
         wa_codes = consts.tile([P, wa_cols], U32, align_bytes=64)
         wa_scales = consts.tile([P, wa_cols], U8, align_bytes=64)
         nc.vector.tensor_copy(out=wa_grouped[:, 0:R_KV, :], in_=wa_raw[:, :, 0:R_KV].rearrange("p t c -> p c t"))
-        nc.vector.quantize_mx(out=wa_codes[:, 0:R_KV].bitcast(FP8X4), scales=wa_scales[:, 0:R_KV],
-                              in_=wa_grouped[:, 0:R_KV, :].rearrange("p c t -> p (c t)"))
         rope_raw = wa_raw[:, :, R_KV:R_KV + D_ROPE]
         raw_pairs = rope_raw.rearrange("p t (i two) -> p i two t", two=2)
         rot_pairs = wa_grouped[:, R_KV + D_ROPE:wa_cols, :].rearrange("p (i two) t -> p i two t", two=2)
@@ -142,8 +141,8 @@ def tile_multiheadlatentattention_pb_t_kernel(tc, x, Wkva, kv_a_norm_w, Wkvb, ou
             nc.vector.quantize_mx(out=wb_codes[:, cols].bitcast(FP8X4), scales=wb_scales[:, cols],
                                   in_=wb_grouped[:, cols, :].rearrange("p c t -> p (c t)"))
 
-        group_wb(0, slice(0, 2))
-        group_wb(0, slice(2, 4))
+        for head in range(HEADS):
+            group_wb(0, slice(head, head + 1))
 
         xh_ps, c_ps, r_ps, sum_sq, inv_rms, h_sb, grouped, xq, hq, prod = {}, {}, {}, {}, {}, {}, {}, {}, {}, {}
         k_sb, v_sb = {}, {}
@@ -250,10 +249,12 @@ def tile_multiheadlatentattention_pb_t_kernel(tc, x, Wkva, kv_a_norm_w, Wkvb, ou
                 nc.sync.dma_start(out=v_groups[b, gs][:, :, i0 * v_w:(last + 1) * v_w],
                                   in_=v_sb[unit][:].rearrange("p h i d -> p h (i d)"))
 
-        def one_step(step):
+        def lay_out(step):
             if live(step + 1) or live(step - 3):
                 transpose_both(step, step + 1, step - 3)
                 group_both(step, step + 1, step - 3)
+
+        def rest_of_step(step):
             if live(step - 1):
                 normalise(step - 1)
             if live(step + 1) or live(step - 3):
@@ -274,14 +275,22 @@ def tile_multiheadlatentattention_pb_t_kernel(tc, x, Wkva, kv_a_norm_w, Wkvb, ou
             if live(step):
                 rope_product(step)
 
-        one_step(-1)
+        def one_step(step):
+            lay_out(step)
+            rest_of_step(step)
+
+        lay_out(-1)
+        nc.vector.quantize_mx(out=wa_codes[:, 0:R_KV].bitcast(FP8X4), scales=wa_scales[:, 0:R_KV],
+                              in_=wa_grouped[:, 0:R_KV, :].rearrange("p c t -> p (c t)"))
+        rest_of_step(-1)
         gain_ps = psum_c.tile([P, R_KV], F32, name="c_ps")
         nc.tensor.matmul(out=gain_ps[:], lhsT=ones[:], rhs=gain_rows[:], start=True, stop=True)
         gain_bc = consts.tile([P, R_KV], BF16)
+        lay_out(0)
         nc.vector.quantize_mx(out=wa_codes[:, R_KV:wa_cols].bitcast(FP8X4), scales=wa_scales[:, R_KV:wa_cols],
                               in_=wa_grouped[:, R_KV:wa_cols, :].rearrange("p c t -> p (c t)"))
         nc.vector.tensor_copy(out=gain_bc[:], in_=gain_ps[:])
-        one_step(0)
+        rest_of_step(0)
         half_sq = trig.tile(shape, F32)
         nc.scalar.activation(out=half_sq[:], in_=half_sin[:], func=ACT.Square)
         nc.scalar.activation(out=cos_sin[:, :, 0, :], in_=half_sq[:], func=ACT.Copy, bias=1.0, scale=-2.0)

import math
from contextlib import ExitStack

import concourse.mybir as mybir
from concourse.masks import make_identity

F32 = mybir.dt.float32
BF16 = mybir.dt.bfloat16
I32 = mybir.dt.int32
U32 = mybir.dt.uint32
U8 = mybir.dt.uint8
FP8X4 = mybir.dt.float8_e4m3fn_x4
ALU = mybir.AluOpType
ACT = mybir.ActivationFunctionType

P = 128
PACK = 4
BATCH, SEQ, D_MODEL, HEADS = 4, 1024, 512, 4
D_NOPE, D_ROPE, D_V, R_KV = 128, 128, 128, 512
ROPE_BASE = 10000.0
EPS = 1e-6

TOKENS = BATCH * SEQ
N_TILES = TOKENS // P
TILES_PER_GROUP = 4
GROUP = P * TILES_PER_GROUP
N_GROUPS = TOKENS // GROUP
GROUPS_PER_SEQ = SEQ // GROUP
TILES_PER_STORE = 2
N_POS = GROUPS_PER_SEQ * TILES_PER_GROUP
N_FREQ = D_ROPE // 2
ROUND_MAGIC = 1.5 * 2.0**23

FLOPS = 2 * TOKENS * D_MODEL * (R_KV + D_ROPE) + 2 * TOKENS * R_KV * HEADS * (D_NOPE + D_V)


def tile_multiheadlatentattention_pb_t_kernel(tc, x, Wkva, kv_a_norm_w, Wkvb, out_0, out_1):
    nc = tc.nc
    x_groups = x.flatten_outer_dims().rearrange("(g p i) k -> g p (i k)", p=P, i=TILES_PER_GROUP)
    k_groups = out_0.rearrange("b h (g p i) d -> b g p h (i d)", p=P, i=TILES_PER_GROUP)
    v_groups = out_1.rearrange("b h (g p i) d -> b g p h (i d)", p=P, i=TILES_PER_GROUP)

    with ExitStack() as ctx:
        ctx.enter_context(tc.manual_schedule())
        consts = ctx.enter_context(tc.tile_pool(name="consts", bufs=1))
        x_pool = ctx.enter_context(tc.tile_pool(name="x_pool", bufs=1))
        trig = ctx.enter_context(tc.tile_pool(name="trig", bufs=1))
        work = ctx.enter_context(tc.tile_pool(name="work", bufs=4))
        small = ctx.enter_context(tc.tile_pool(name="small", bufs=8))
        outs = ctx.enter_context(tc.tile_pool(name="outs", bufs=6))
        psum_xh = ctx.enter_context(tc.psum_pool(name="psum_xh", bufs=1))
        psum_c = ctx.enter_context(tc.psum_pool(name="psum_c", bufs=2))
        psum_r = ctx.enter_context(tc.psum_pool(name="psum_r", bufs=2))
        psum_kv = ctx.enter_context(tc.psum_pool(name="psum_kv", bufs=3))

        pos_i = consts.tile([P, N_POS], I32)
        nc.gpsimd.iota(pos_i[:], pattern=[[GROUP, GROUPS_PER_SEQ], [1, TILES_PER_GROUP]], base=0,
                       channel_multiplier=TILES_PER_GROUP)
        ident_f32 = consts.tile([P, P], F32)
        make_identity(nc, ident_f32[:])
        gain_rows = consts.tile([P, R_KV], BF16)
        nc.gpsimd.memset(gain_rows[:].bitcast(F32), 0.0)

        wa_raw = consts.tile([P, PACK, R_KV + D_ROPE], BF16)
        nc.sync.dma_start(
            out=wa_raw[:].rearrange("q (u e) c -> q u (e c)", u=2),
            in_=Wkva.rearrange("(u q e) c -> q u (e c)", u=2, e=2),
        )
        wb_raw = consts.tile([P, PACK, HEADS * (D_NOPE + D_V)], BF16)
        x_sb = []
        for g in range(N_GROUPS):
            x_tile = x_pool.tile([P, TILES_PER_GROUP * D_MODEL], BF16, name="x_sb%d" % g)
            nc.sync.dma_start(out=x_tile[:], in_=x_groups[g])
            x_sb.append(x_tile)
            if g == 0:
                nc.sync.dma_start(out=gain_rows[0:1, :], in_=kv_a_norm_w.rearrange("(o k) -> o k", o=1))
                nc.sync.dma_start(
                    out=wb_raw[:].rearrange("q (u e) c -> q u (e c)", u=2),
                    in_=Wkvb.rearrange("(u q e) c -> q u (e c)", u=2, e=2),
                )

        ones = consts.tile([P, P], BF16)
        nc.gpsimd.memset(ones[:], 1.0)
        eps_col = consts.tile([P, 1], F32)
        nc.gpsimd.memset(eps_col[:], EPS)

        shape = [P, N_POS, N_FREQ]
        turns = trig.tile(shape, F32)
        nc.vector.tensor_scalar(out=turns[:, :, 0:1], in0=pos_i[:].unsqueeze(2), scalar1=0.5 / math.pi, scalar2=None,
                                op0=ALU.mult)
        for level in range(3):
            have = 4**level
            for m in (1, 2, 3):
                nc.vector.tensor_scalar(out=turns[:, :, m * have:(m + 1) * have], in0=turns[:, :, 0:have],
                                        scalar1=ROPE_BASE ** (-m * have / N_FREQ), scalar2=None, op0=ALU.mult)
        whole = trig.tile(shape, F32)
        nc.vector.tensor_scalar(out=whole[:], in0=turns[:], scalar1=ROUND_MAGIC, scalar2=ROUND_MAGIC,
                                op0=ALU.add, op1=ALU.subtract)
        part = trig.tile(shape, F32)
        nc.vector.tensor_tensor(out=part[:], in0=turns[:], in1=whole[:], op=ALU.subtract)
        cos_sin = consts.tile([P, N_POS, 2, N_FREQ], F32)
        nc.scalar.activation(out=cos_sin[:, :, 1, :], in_=part[:], func=ACT.Sin, scale=2.0 * math.pi)
        half_sin = trig.tile(shape, F32)
        nc.scalar.activation(out=half_sin[:], in_=part[:], func=ACT.Sin, scale=math.pi)
        table_warmer = trig.tile([P, 1], F32)
        nc.scalar.activation(out=table_warmer[:], in_=eps_col[:], func=ACT.Abs_reciprocal_sqrt)

        wa_cols = R_KV + 2 * D_ROPE
        wa_grouped = consts.tile([P, wa_cols, PACK], BF16, align_bytes=64)
        wa_codes = consts.tile([P, wa_cols], U32, align_bytes=64)
        wa_scales = consts.tile([P, wa_cols], U8, align_bytes=64)
        nc.vector.tensor_copy(out=wa_grouped[:, 0:R_KV, :], in_=wa_raw[:, :, 0:R_KV].rearrange("p t c -> p c t"))
        rope_raw = wa_raw[:, :, R_KV:R_KV + D_ROPE]
        raw_pairs = rope_raw.rearrange("p t (i two) -> p i two t", two=2)
        rot_pairs = wa_grouped[:, R_KV + D_ROPE:wa_cols, :].rearrange("p (i two) t -> p i two t", two=2)
        nc.gpsimd.tensor_scalar(out=wa_grouped[:, R_KV:R_KV + D_ROPE, :], in0=rope_raw.rearrange("p t c -> p c t"),
                                scalar1=1.0, scalar2=0.0, op0=ALU.mult, op1=ALU.add)
        nc.gpsimd.tensor_scalar(out=rot_pairs[:, :, 0, :], in0=raw_pairs[:, :, 1, :], scalar1=-1.0, scalar2=0.0,
                                op0=ALU.mult, op1=ALU.add)
        nc.gpsimd.tensor_scalar(out=rot_pairs[:, :, 1, :], in0=raw_pairs[:, :, 0, :], scalar1=1.0, scalar2=0.0,
                                op0=ALU.mult, op1=ALU.add)

        wb_cols = HEADS * (D_NOPE + D_V)
        half_cols = wb_cols // 2
        wb_grouped = consts.tile([P, wb_cols, PACK], BF16, align_bytes=64)
        wb_codes = consts.tile([P, wb_cols], U32, align_bytes=64)
        wb_scales = consts.tile([P, wb_cols], U8, align_bytes=64)
        wb_parts = wb_raw[:].rearrange("p t (h kv d) -> p kv h d t", kv=2, d=D_NOPE)

        def group_wb(kv, heads):
            cols = slice(kv * half_cols, (kv + 1) * half_cols)
            dst = wb_grouped[:, cols, :].rearrange("p (h d) t -> p h d t", h=HEADS)
            if kv == 0:
                nc.gpsimd.tensor_scalar(out=dst[:, heads], in0=wb_parts[:, kv, heads], scalar1=1.0, scalar2=0.0,
                                        op0=ALU.mult, op1=ALU.add)
            else:
                nc.scalar.copy(out=dst[:, heads], in_=wb_parts[:, kv, heads])

        def quantise_wb(kv):
            cols = slice(kv * half_cols, (kv + 1) * half_cols)
            nc.vector.quantize_mx(out=wb_codes[:, cols].bitcast(FP8X4), scales=wb_scales[:, cols],
                                  in_=wb_grouped[:, cols, :].rearrange("p c t -> p (c t)"))

        for head in range(HEADS):
            group_wb(0, slice(head, head + 1))

        xh_ps, c_ps, r_ps, sum_sq, inv_rms, h_sb, grouped, xq, hq, prod = {}, {}, {}, {}, {}, {}, {}, {}, {}, {}
        k_sb, v_sb = {}, {}

        def live(n):
            return 0 <= n < N_TILES

        def transpose_both(step, nx, nh):
            xh_ps[step] = psum_xh.tile([P, 4, P], F32, name="xh_ps")
            if live(nx):
                g, i = divmod(nx, TILES_PER_GROUP)
                words = x_sb[g][:].bitcast(F32)
                for u in range(2):
                    first = (i * 2 + u) * P
                    nc.tensor.transpose(xh_ps[step][:, u, :], words[:, first:first + P], ident_f32[:])
            if live(nh):
                words = h_sb[nh][:].bitcast(F32)
                for u in range(2):
                    nc.tensor.transpose(xh_ps[step][:, 2 + u, :], words[:, u * P:(u + 1) * P], ident_f32[:])

        def group_both(step, nx, nh):
            grouped[step] = work.tile([P, 2 * P * PACK], BF16, name="grouped", align_bytes=64)
            lo = 0 if live(nx) else 2
            hi = 4 if live(nh) else 2
            nc.vector.tensor_copy(
                out=grouped[step][:].bitcast(F32)[:, lo * P:hi * P].rearrange("p (w n u) -> p w n u", n=P, u=2),
                in_=xh_ps[step][:, lo:hi, :].rearrange("p (w u) n -> p w n u", u=2))

        def quantise_both(step, nx, nh):
            codes = work.tile([P, 2 * P], U32, name="codes", align_bytes=64)
            scales = work.tile([P, 2 * P], U8, name="scales", align_bytes=64)
            lo = 0 if live(nx) else P
            hi = 2 * P if live(nh) else P
            nc.vector.quantize_mx(out=codes[:, lo:hi].bitcast(FP8X4), scales=scales[:, lo:hi],
                                  in_=grouped[step][:, lo * PACK:hi * PACK])
            xq[nx] = (codes[:, 0:P], scales[:, 0:P])
            hq[nh] = (codes[:, P:2 * P], scales[:, P:2 * P])

        def latent_product(n):
            codes, scales = xq[n]
            c_ps[n] = psum_c.tile([P, R_KV], F32, name="c_ps")
            nc.tensor.matmul_mx(out=c_ps[n][:], lhsT=codes.bitcast(FP8X4), lhsT_scale=scales,
                                rhs=wa_codes[:, 0:R_KV].bitcast(FP8X4), rhs_scale=wa_scales[:, 0:R_KV],
                                start=True, stop=True)

        def rope_product(n):
            codes, scales = xq[n]
            r_ps[n] = psum_r.tile([P, 2 * D_ROPE], F32, name="r_ps")
            nc.tensor.matmul_mx(out=r_ps[n][:], lhsT=codes.bitcast(FP8X4), lhsT_scale=scales,
                                rhs=wa_codes[:, R_KV:wa_cols].bitcast(FP8X4), rhs_scale=wa_scales[:, R_KV:wa_cols],
                                start=True, stop=True)

        def sum_squares(n):
            squares = work.tile([P, R_KV], BF16, name="squares")
            sum_sq[n] = small.tile([P, 1], F32, name="sum_sq")
            nc.scalar.activation(out=squares[:], in_=c_ps[n][:], func=ACT.Square, accum_out=sum_sq[n][:])

        def invert_rms(n):
            inv_rms[n] = small.tile([P, 1], F32, name="inv_rms")
            nc.scalar.activation(out=inv_rms[n][:], in_=sum_sq[n][:], func=ACT.Abs_reciprocal_sqrt, bias=eps_col[:],
                                 scale=1.0 / R_KV)

        def normalise(n):
            h_sb[n] = work.tile([P, R_KV], BF16, name="h_sb")
            nc.vector.scalar_tensor_tensor(out=h_sb[n][:], in0=c_ps[n][:], scalar=inv_rms[n][:], in1=gain_bc[:],
                                           op0=ALU.mult, op1=ALU.mult)

        def rotate(n):
            twice = [P, 2, 2, N_FREQ]
            prod[n] = work.tile(twice, F32, name="prod")
            nc.vector.tensor_tensor(out=prod[n][:], in0=r_ps[n][:].rearrange("p (c r j) -> p c r j", c=2, r=2),
                                    in1=cos_sin[:, n % N_POS].unsqueeze(2).to_broadcast(twice), op=ALU.mult)

        def spread(n):
            unit, j = divmod(n, TILES_PER_STORE)
            if j == 0:
                k_sb[unit] = outs.tile([P, HEADS, TILES_PER_STORE, D_NOPE + D_ROPE], F32, name="k_sb")
                v_sb[unit] = outs.tile([P, HEADS, TILES_PER_STORE, D_V], F32, name="v_sb")
            first = k_sb[unit][:, 0, j, D_NOPE:D_NOPE + D_ROPE]
            nc.vector.tensor_tensor(out=first, in0=prod[n][:, 0].rearrange("p r j -> p (r j)"),
                                    in1=prod[n][:, 1].rearrange("p r j -> p (r j)"), op=ALU.add)
            nc.gpsimd.tensor_scalar(out=k_sb[unit][:, 1:HEADS, j, D_NOPE:D_NOPE + D_ROPE],
                                    in0=first.unsqueeze(1).to_broadcast([P, HEADS - 1, D_ROPE]),
                                    scalar1=1.0, scalar2=0.0, op0=ALU.mult, op1=ALU.add)

        def second_product(n, kv_range):
            unit, j = divmod(n, TILES_PER_STORE)
            codes, scales = hq[n]
            for kv in kv_range:
                cols = slice(kv * half_cols, (kv + 1) * half_cols)
                kv_ps = psum_kv.tile([P, half_cols], F32, name="kv_ps")
                nc.tensor.matmul_mx(out=kv_ps[:], lhsT=codes.bitcast(FP8X4), lhsT_scale=scales,
                                    rhs=wb_codes[:, cols].bitcast(FP8X4), rhs_scale=wb_scales[:, cols],
                                    start=True, stop=True)
                dst = k_sb[unit][:, :, j, 0:D_NOPE] if kv == 0 else v_sb[unit][:, :, j, :]
                nc.scalar.copy(out=dst, in_=kv_ps[:].rearrange("p (h d) -> p h d", h=HEADS))
            if j == TILES_PER_STORE - 1 and 1 in kv_range:
                g, last = divmod(n, TILES_PER_GROUP)
                b, gs = divmod(g, GROUPS_PER_SEQ)
                i0 = last + 1 - TILES_PER_STORE
                k_w, v_w = D_NOPE + D_ROPE, D_V
                nc.sync.dma_start(out=k_groups[b, gs][:, :, i0 * k_w:(last + 1) * k_w],
                                  in_=k_sb[unit][:].rearrange("p h i d -> p h (i d)"))
                nc.sync.dma_start(out=v_groups[b, gs][:, :, i0 * v_w:(last + 1) * v_w],
                                  in_=v_sb[unit][:].rearrange("p h i d -> p h (i d)"))

        def lay_out(step):
            if live(step + 1) or live(step - 3):
                transpose_both(step, step + 1, step - 3)
                group_both(step, step + 1, step - 3)

        def rest_of_step(step):
            if live(step - 1):
                normalise(step - 1)
            if live(step + 1) or live(step - 3):
                quantise_both(step, step + 1, step - 3)
            if live(step - 2):
                spread(step - 2)
            if live(step - 1):
                rotate(step - 1)
            if live(step):
                latent_product(step)
                sum_squares(step)
            if live(step - 4):
                second_product(step - 4, (0,))
            if live(step):
                invert_rms(step)
            if live(step - 4):
                second_product(step - 4, (1,))
            if live(step):
                rope_product(step)

        def one_step(step):
            lay_out(step)
            rest_of_step(step)

        lay_out(-1)
        nc.vector.quantize_mx(out=wa_codes[:, 0:R_KV].bitcast(FP8X4), scales=wa_scales[:, 0:R_KV],
                              in_=wa_grouped[:, 0:R_KV, :].rearrange("p c t -> p (c t)"))
        rest_of_step(-1)
        gain_ps = psum_c.tile([P, R_KV], F32, name="c_ps")
        nc.tensor.matmul(out=gain_ps[:], lhsT=ones[:], rhs=gain_rows[:], start=True, stop=True)
        gain_bc = consts.tile([P, R_KV], BF16)
        lay_out(0)
        nc.vector.quantize_mx(out=wa_codes[:, R_KV:wa_cols].bitcast(FP8X4), scales=wa_scales[:, R_KV:wa_cols],
                              in_=wa_grouped[:, R_KV:wa_cols, :].rearrange("p c t -> p (c t)"))
        nc.vector.tensor_copy(out=gain_bc[:], in_=gain_ps[:])
        rest_of_step(0)
        half_sq = trig.tile(shape, F32)
        nc.scalar.activation(out=half_sq[:], in_=half_sin[:], func=ACT.Square)
        nc.scalar.activation(out=cos_sin[:, :, 0, :], in_=half_sq[:], func=ACT.Copy, bias=1.0, scale=-2.0)
        one_step(1)
        group_wb(1, slice(0, 2))
        one_step(2)
        group_wb(1, slice(2, 4))
        quantise_wb(0)
        one_step(3)
        quantise_wb(1)
        for step in range(4, N_TILES + 4):
            one_step(step)
